import numpy as np
import ml_dtypes


def mxq(x, axis, fmt="e4m3"):
    dtype, down = {"e4m3": (ml_dtypes.float8_e4m3fn, 7), "e5m2": (ml_dtypes.float8_e5m2, 14)}[fmt]
    v = np.moveaxis(np.asarray(x, np.float32).astype(ml_dtypes.bfloat16).astype(np.float64), axis, -1)
    blocks = v.reshape(v.shape[:-1] + (-1, 32))
    amax = np.abs(blocks).max(-1, keepdims=True)
    byte = np.maximum(np.where(amax > 0, np.frexp(amax)[1] - 1 + 127, 0) - down, 1)
    scale = np.exp2(byte - 127.0)
    codes = (blocks / scale).astype(np.float32).astype(dtype).astype(np.float64)
    return np.moveaxis((codes * scale).reshape(v.shape), -1, axis)


WIDE = False


def mx_kscale(k):
    if not WIDE:
        return np.ones(k)
    levels = np.array([10, -10, 5, -5, 0])
    a = np.random.permutation(np.resize(levels, k // 512 * 4)).reshape(k // 512, 4)
    idx = np.arange(k)
    return np.exp2(a[idx // 512, idx % 128 // 32])


BF16 = ml_dtypes.bfloat16


def bf(x):
    return np.asarray(x, np.float32).astype(BF16)


def f64(x):
    return np.asarray(x).astype(np.float64)


T, DIM, NH, HD = 512, 2048, 16, 128


def setup_inputs():
    s = mx_kscale(DIM)
    return {"x": bf(np.random.standard_normal((T, DIM)) * s),
            "Wv": bf(np.random.standard_normal((NH * HD, DIM)) * DIM ** -0.5 / s[None, :]),
            "vi": bf(np.random.standard_normal((T, NH, HD))),
            "lamb": bf(0.25 + 0.5 * np.random.random(1)),
            "q_rot": bf(np.random.standard_normal((T, NH, HD))),
            "k_rot": bf(np.random.standard_normal((T, NH, HD)))}


def reference(x, Wv, vi, lamb, q_rot, k_rot):
    lam = f64(lamb)[0]
    v = (mxq(f64(x), 1, "e4m3") @ mxq(f64(Wv), 1, "e4m3").T).reshape(T, NH, HD)
    v = (1.0 - lam) * v + lam * f64(vi)
    s = (f64(q_rot).transpose(1, 0, 2) @ f64(k_rot).transpose(1, 2, 0)) * HD ** -0.5
    causal = np.tril(np.ones((T, T), dtype=bool))
    s = np.where(causal[None], s, -np.inf)
    e = np.exp(s - s.max(-1, keepdims=True))
    y = (mxq(e, 2, "e4m3") @ mxq(v.transpose(1, 0, 2), 1, "e4m3")) / e.sum(-1, keepdims=True)
    return y.transpose(1, 0, 2)

@@ -1,0 +1,362 @@
+from contextlib import ExitStack
+
+import concourse.masks as masks
+import concourse.mybir as mybir
+
+F32 = mybir.dt.float32
+BF16 = mybir.dt.bfloat16
+U32 = mybir.dt.uint32
+U8 = mybir.dt.uint8
+FP8X4 = mybir.dt.float8_e4m3fn_x4
+ALU = mybir.AluOpType
+ACT = mybir.ActivationFunctionType
+AXIS = mybir.AxisListType
+
+P = 128
+PACK = 4
+K_PASS = P * PACK
+TOKENS = 512
+DIM = 2048
+HEADS = 16
+HEAD_DIM = 128
+TOKEN_TILES = TOKENS // P
+K_PASSES = DIM // K_PASS
+WORDS = K_PASS // 2
+BANK = 512
+SCALE = HEAD_DIM ** -0.5
+MASKED = -1.0e30
+
+HEADS_PER_LOAD = 4
+LOAD_COLS = HEADS_PER_LOAD * HEAD_DIM
+
+LEAD = 2
+E_TILES = 3
+
+FLOPS = 2 * TOKENS * DIM * DIM + 2 * 2 * HEADS * TOKENS * TOKENS * HEAD_DIM
+
+
+def tile_causalselfattention_pb_kernel(tc, x, Wv, vi, lamb, q_rot, k_rot, out):
+    nc = tc.nc
+    with ExitStack() as ctx:
+        ctx.enter_context(tc.manual_schedule())
+
+        consts = ctx.enter_context(tc.tile_pool(name="consts", bufs=1))
+        inputs = ctx.enter_context(tc.tile_pool(name="inputs", bufs=1))
+        x_mx = ctx.enter_context(tc.tile_pool(name="x_mx", bufs=1))
+        grouped_pool = ctx.enter_context(tc.tile_pool(name="grouped", bufs=4))
+        w_mx = ctx.enter_context(tc.tile_pool(name="w_mx", bufs=3))
+        e_mx = ctx.enter_context(tc.tile_pool(name="e_mx", bufs=LEAD + 3))
+        v_mx = ctx.enter_context(tc.tile_pool(name="v_mx", bufs=3))
+        qk_pool = ctx.enter_context(tc.tile_pool(name="qk", bufs=3))
+        rows = ctx.enter_context(tc.tile_pool(name="rows", bufs=LEAD + 5))
+        work = ctx.enter_context(tc.tile_pool(name="work", bufs=3))
+        transposed = ctx.enter_context(tc.psum_pool(name="transposed", bufs=3))
+        score_banks = ctx.enter_context(tc.psum_pool(name="scores", bufs=3))
+        sums = ctx.enter_context(tc.psum_pool(name="sums", bufs=2))
+
+        q_view = q_rot.rearrange("(i p) h d -> p i (h d)", p=P)
+        k_view = k_rot.rearrange("(i p) h d -> p i (h d)", p=P)
+        x_view = x.rearrange("(half p odd) k -> p half (odd k)", half=2, odd=2)
+        vi_view = vi.rearrange("(half p odd) h d -> p half odd (h d)", half=2, odd=2)
+        out_view = out.rearrange("(i p) h d -> p i h d", p=P)
+
+        lamb_bf16 = consts.tile([P, 1], BF16, name="lamb_bf16")
+        nc.scalar.dma_start(out=lamb_bf16[:], in_=lamb.partition_broadcast(P))
+
+        x_raw = inputs.tile([P, TOKEN_TILES * DIM], BF16, name="x_raw")
+        q_raw, k_raw, vi_raw, w_raw = {}, {}, {}, {}
+
+        def starts_a_load(head):
+            return 0 <= head < HEADS and head % HEADS_PER_LOAD == 0
+
+        first_step = -(LEAD + 2)
+        last_step = HEADS + 2
+        x_step = -2
+
+        for step in range(first_step, last_step):
+            head = step + LEAD + 2
+            if starts_a_load(head):
+                group = head // HEADS_PER_LOAD
+                cols = slice(group * LOAD_COLS, (group + 1) * LOAD_COLS)
+                q_raw[group] = inputs.tile([P, TOKEN_TILES, LOAD_COLS], BF16, name="q_raw%d" % group)
+                k_raw[group] = inputs.tile([P, TOKEN_TILES, LOAD_COLS], BF16, name="k_raw%d" % group)
+                nc.sync.dma_start(out=q_raw[group][:], in_=q_view[:, :, cols])
+                nc.sync.dma_start(out=k_raw[group][:], in_=k_view[:, :, cols])
+            if step == x_step:
+                x_halves = x_raw[:].rearrange("p (half r) -> p half r", half=2)
+                for half in range(2):
+                    nc.sync.dma_start(out=x_halves[:, half, :], in_=x_view[:, half, :])
+            head = step + 2
+            if 0 <= head < HEADS:
+                w_raw[head] = inputs.tile([P, DIM], BF16, name="w_raw%d" % head)
+                nc.sync.dma_start(out=w_raw[head][:], in_=Wv[head * P : (head + 1) * P, :])
+            head = step + 1
+            if starts_a_load(head):
+                group = head // HEADS_PER_LOAD
+                cols = slice(group * LOAD_COLS, (group + 1) * LOAD_COLS)
+                vi_raw[group] = inputs.tile([P, PACK, LOAD_COLS], BF16, name="vi_raw%d" % group)
+                for half in range(2):
+                    nc.sync.dma_start(
+                        out=vi_raw[group][:, 2 * half : 2 * half + 2, :],
+                        in_=vi_view[:, half, :, cols],
+                    )
+
+        ident_f32 = consts.tile([P, P], F32, name="ident_f32")
+        masks.make_identity(nc, ident_f32[:])
+        ident_bf16 = consts.tile([P, P], BF16, name="ident_bf16")
+        masks.make_identity(nc, ident_bf16[:])
+        mask_f32 = consts.tile([P, P], F32, name="mask_f32")
+        nc.gpsimd.memset(mask_f32[:], 0.0)
+        nc.gpsimd.affine_select(
+            out=mask_f32[:],
+            in_=mask_f32[:],
+            compare_op=ALU.is_ge,
+            fill=MASKED,
+            base=0,
+            pattern=[[-1, P]],
+            channel_multiplier=1,
+        )
+        e_tiles = []
+        for n in range(E_TILES):
+            e_tile = consts.tile([P, TOKEN_TILES * TOKENS], BF16, name="e_tile%d" % n)
+            nc.vector.memset(e_tile[:], 0.0)
+            e_tiles.append(e_tile)
+        future_mask = consts.tile([P, P], BF16, name="future_mask")
+        nc.vector.tensor_copy(out=future_mask[:], in_=mask_f32[:])
+        lam = consts.tile([P, 1], F32, name="lam")
+        nc.vector.tensor_copy(out=lam[:], in_=lamb_bf16[:])
+        one_minus_lam = consts.tile([P, 1], F32, name="one_minus_lam")
+        nc.vector.tensor_scalar(
+            out=one_minus_lam[:], in0=lam[:], scalar1=-1.0, scalar2=1.0, op0=ALU.mult, op1=ALU.add
+        )
+
+        def pairs_onto_partitions(source_words, name, copy_first, copy_second):
+            grouped = grouped_pool.tile([P, PACK * BANK], BF16, name=name, tag="grouped", align_bytes=64)
+            grouped_words = grouped[:].bitcast(F32).rearrange(
+                "p (run row half) -> p run row half", run=4, half=2
+            )
+            for pair, copy_out in enumerate((copy_first, copy_second)):
+                bank = transposed.tile([P, 2, 2, P], F32, name="word_bank", tag="transposed")
+                for run in range(2):
+                    for half in range(2):
+                        nc.tensor.transpose(
+                            bank[:, run, half, :],
+                            source_words[:, 2 * pair + run, half * P : (half + 1) * P],
+                            ident_f32[:],
+                        )
+                copy_out(
+                    out=grouped_words[:, 2 * pair : 2 * pair + 2],
+                    in_=bank[:].rearrange("p run half row -> p run row half"),
+                )
+            return grouped
+
+        def quantise(grouped, codes, scales):
+            nc.vector.quantize_mx(out=codes.bitcast(FP8X4), scales=scales, in_=grouped[:])
+
+        x_codes = x_mx.tile([P, K_PASSES, TOKENS], U32, name="x_codes", align_bytes=64)
+        x_scales = x_mx.tile([P, K_PASSES, TOKENS], U8, name="x_scales", align_bytes=64)
+
+        def quantise_activations():
+            x_words = x_raw[:].bitcast(F32).rearrange("p (j w) -> p j w", j=TOKEN_TILES)
+            waiting = {}
+            for c in range(K_PASSES + 1):
+                if c < K_PASSES:
+                    waiting[c] = pairs_onto_partitions(
+                        x_words[:, :, c * WORDS : (c + 1) * WORDS],
+                        "x_grouped",
+                        nc.vector.tensor_copy,
+                        nc.scalar.copy,
+                    )
+                if c > 0:
+                    quantise(waiting[c - 1], x_codes[:, c - 1, :], x_scales[:, c - 1, :])
+
+        w_grouped, w_codes, w_scales = {}, {}, {}
+        qk_t = {}
+        e_grouped, e_codes, e_scales = {}, {}, {}
+        row_sum, row_scale = {}, {}
+        residual, v_sum, v_codes, v_scales = {}, {}, {}, {}
+        y_sum = {}
+
+        def transpose_weights(head):
+            w_words = w_raw[head][:].bitcast(F32).rearrange("p (c w) -> p c w", c=K_PASSES)
+            w_grouped[head] = pairs_onto_partitions(w_words, "w_grouped", nc.scalar.copy, nc.scalar.copy)
+
+        def quantise_weights(head):
+            w_codes[head] = w_mx.tile([P, K_PASSES * HEAD_DIM], U32, name="w_codes", align_bytes=64)
+            w_scales[head] = w_mx.tile([P, K_PASSES * HEAD_DIM], U8, name="w_scales", align_bytes=64)
+            quantise(w_grouped[head], w_codes[head][:], w_scales[head][:])
+
+        def project_values(head):
+            v_sum[head] = sums.tile([P, PACK, HEAD_DIM], F32, name="v_sum", tag="sums")
+            for j in range(TOKEN_TILES):
+                for c in range(K_PASSES):
+                    tokens = slice(j * P, (j + 1) * P)
+                    features = slice(c * HEAD_DIM, (c + 1) * HEAD_DIM)
+                    nc.tensor.matmul_mx(
+                        out=v_sum[head][:, j, :],
+                        lhsT=x_codes[:, c, tokens].bitcast(FP8X4),
+                        lhsT_scale=x_scales[:, c, tokens],
+                        rhs=w_codes[head][:, features].bitcast(FP8X4),
+                        rhs_scale=w_scales[head][:, features],
+                        start=(c == 0),
+                        stop=(c == K_PASSES - 1),
+                    )
+
+        def scale_residual(head):
+            group = head // HEADS_PER_LOAD
+            cols = slice((head % HEADS_PER_LOAD) * HEAD_DIM, (head % HEADS_PER_LOAD + 1) * HEAD_DIM)
+            residual[head] = work.tile([P, HEAD_DIM, PACK], F32, name="residual")
+            nc.gpsimd.tensor_scalar(
+                out=residual[head][:],
+                in0=vi_raw[group][:, :, cols].rearrange("p j d -> p d j"),
+                scalar1=lam[:, 0:1],
+                scalar2=0.0,
+                op0=ALU.mult,
+                op1=ALU.add,
+            )
+
+        def mix_values(head):
+            v_grouped = work.tile([P, HEAD_DIM, PACK], BF16, name="v_grouped", align_bytes=64)
+            nc.vector.scalar_tensor_tensor(
+                out=v_grouped[:],
+                in0=v_sum[head][:].rearrange("p j d -> p d j"),
+                scalar=one_minus_lam[:, 0:1],
+                in1=residual[head][:],
+                op0=ALU.mult,
+                op1=ALU.add,
+            )
+            return v_grouped
+
+        def quantise_values(head, v_grouped):
+            v_codes[head] = v_mx.tile([P, HEAD_DIM], U32, name="v_codes", align_bytes=64)
+            v_scales[head] = v_mx.tile([P, HEAD_DIM], U8, name="v_scales", align_bytes=64)
+            nc.vector.quantize_mx(
+                out=v_codes[head][:].bitcast(FP8X4),
+                scales=v_scales[head][:],
+                in_=v_grouped[:].rearrange("p d j -> p (d j)"),
+            )
+
+        def transpose_queries_keys(head):
+            group = head // HEADS_PER_LOAD
+            cols = slice((head % HEADS_PER_LOAD) * HEAD_DIM, (head % HEADS_PER_LOAD + 1) * HEAD_DIM)
+            bank = transposed.tile([P, 2, TOKENS], BF16, name="qk_bank", tag="transposed")
+            for which, raw in enumerate((q_raw[group], k_raw[group])):
+                for i in range(TOKEN_TILES):
+                    nc.tensor.transpose(bank[:, which, i * P : (i + 1) * P], raw[:, i, cols], ident_bf16[:])
+            qk_t[head] = qk_pool.tile([P, 2, TOKENS], BF16, name="qk_t")
+            nc.scalar.copy(out=qk_t[head][:], in_=bank[:])
+
+        def scores_and_exponentials(head):
+            even_bank = score_banks.tile([P, BANK], F32, name="even_bank", tag="scores")
+            bank_1 = score_banks.tile([P, BANK], F32, name="bank_1", tag="scores")
+            bank_3 = score_banks.tile([P, BANK], F32, name="bank_3", tag="scores")
+            score = {
+                0: even_bank[:, 3 * P : 4 * P],
+                2: even_bank[:, 0 : 3 * P],
+                1: bank_1[:, 0 : 2 * P],
+                3: bank_3[:, 0 : 4 * P],
+            }
+            for i in (0, 2, 1, 3):
+                keys = (i + 1) * P
+                nc.tensor.matmul(
+                    out=score[i],
+                    lhsT=qk_t[head][:, 0, i * P : (i + 1) * P],
+                    rhs=qk_t[head][:, 1, 0:keys],
+                    start=True,
+                    stop=False,
+                )
+                nc.tensor.matmul(
+                    out=score[i][:, keys - P : keys],
+                    lhsT=ident_bf16[:],
+                    rhs=future_mask[:],
+                    start=False,
+                    stop=True,
+                )
+            neg_max = rows.tile([P, TOKEN_TILES], F32, name="neg_max")
+            shift = rows.tile([P, TOKEN_TILES], F32, name="shift")
+            row_sum[head] = rows.tile([P, TOKEN_TILES], F32, name="row_sum")
+            e_rows = e_tiles[head % E_TILES][:].rearrange("p (i u) -> p i u", i=TOKEN_TILES)
+            for parity in range(2):
+                pair = (parity, parity + 2)
+                both = slice(parity, TOKEN_TILES, 2)
+                for i in pair:
+                    nc.vector.tensor_reduce(
+                        out=neg_max[:, i : i + 1], in_=score[i], axis=AXIS.X, op=ALU.max, negate=True
+                    )
+                nc.vector.tensor_scalar(
+                    out=shift[:, both], in0=neg_max[:, both], scalar1=SCALE, scalar2=None, op0=ALU.mult
+                )
+                for i in pair:
+                    nc.scalar.activation(
+                        out=e_rows[:, i, 0 : (i + 1) * P],
+                        in_=score[i],
+                        func=ACT.Exp,
+                        bias=shift[:, i : i + 1],
+                        scale=SCALE,
+                        accum_out=row_sum[head][:, i : i + 1],
+                    )
+
+        def transpose_probabilities(head):
+            e_words = e_tiles[head % E_TILES][:].bitcast(F32).rearrange("p (i w) -> p i w", i=TOKEN_TILES)
+            e_grouped[head] = pairs_onto_partitions(e_words, "e_grouped", nc.scalar.copy, nc.scalar.copy)
+
+        def quantise_probabilities(head):
+            e_codes[head] = e_mx.tile([P, TOKENS], U32, name="e_codes", align_bytes=64)
+            e_scales[head] = e_mx.tile([P, TOKENS], U8, name="e_scales", align_bytes=64)
+            quantise(e_grouped[head], e_codes[head][:], e_scales[head][:])
+            row_scale[head] = rows.tile([P, TOKEN_TILES], F32, name="row_scale")
+            nc.vector.reciprocal(out=row_scale[head][:], in_=row_sum[head][:])
+
+        def attend(head):
+            y_sum[head] = sums.tile([P, TOKEN_TILES, HEAD_DIM], F32, name="y_sum", tag="sums")
+            for i in range(TOKEN_TILES):
+                queries = slice(i * P, (i + 1) * P)
+                nc.tensor.matmul_mx(
+                    out=y_sum[head][:, i, :],
+                    lhsT=e_codes[head][:, queries].bitcast(FP8X4),
+                    lhsT_scale=e_scales[head][:, queries],
+                    rhs=v_codes[head][:].bitcast(FP8X4),
+                    rhs_scale=v_scales[head][:],
+                    start=True,
+                    stop=True,
+                )
+
+        def normalise_and_store(head):
+            y = work.tile([P, TOKEN_TILES, HEAD_DIM], F32, name="y")
+            nc.vector.tensor_tensor(
+                out=y[:],
+                in0=y_sum[head][:],
+                in1=row_scale[head][:].unsqueeze(2).to_broadcast([P, TOKEN_TILES, HEAD_DIM]),
+                op=ALU.mult,
+            )
+            nc.sync.dma_start(out=out_view[:, :, head, :], in_=y[:])
+
+        def live(head):
+            return 0 <= head < HEADS
+
+        for step in range(first_step, last_step):
+            if step == x_step:
+                quantise_activations()
+            if live(step + 2):
+                transpose_weights(step + 2)
+            if live(step + LEAD + 2):
+                transpose_queries_keys(step + LEAD + 2)
+            if live(step + LEAD):
+                transpose_probabilities(step + LEAD)
+            if live(step + 1):
+                scale_residual(step + 1)
+            v_grouped = mix_values(step) if live(step) else None
+            if live(step - 2):
+                normalise_and_store(step - 2)
+            if live(step):
+                quantise_values(step, v_grouped)
+            if live(step + 2):
+                quantise_weights(step + 2)
+            if live(step + LEAD + 1):
+                scores_and_exponentials(step + LEAD + 1)
+            if live(step + LEAD):
+                quantise_probabilities(step + LEAD)
+            if live(step + 1):
+                project_values(step + 1)
+            if live(step - 1):
+                attend(step - 1)

@@ -29,7 +29,7 @@ MASKED = -1.0e30
 HEADS_PER_LOAD = 4
 LOAD_COLS = HEADS_PER_LOAD * HEAD_DIM
 
-LEAD = 2
+LEAD = 1
 E_TILES = 3
 
 FLOPS = 2 * TOKENS * DIM * DIM + 2 * 2 * HEADS * TOKENS * TOKENS * HEAD_DIM
@@ -48,10 +48,11 @@ def tile_causalselfattention_pb_kernel(tc, x, Wv, vi, lamb, q_rot, k_rot, out):
         e_mx = ctx.enter_context(tc.tile_pool(name="e_mx", bufs=LEAD + 3))
         v_mx = ctx.enter_context(tc.tile_pool(name="v_mx", bufs=3))
         qk_pool = ctx.enter_context(tc.tile_pool(name="qk", bufs=3))
+        scaled_pool = ctx.enter_context(tc.tile_pool(name="scaled", bufs=2))
         rows = ctx.enter_context(tc.tile_pool(name="rows", bufs=LEAD + 5))
         work = ctx.enter_context(tc.tile_pool(name="work", bufs=3))
-        transposed = ctx.enter_context(tc.psum_pool(name="transposed", bufs=3))
-        score_banks = ctx.enter_context(tc.psum_pool(name="scores", bufs=3))
+        transposed = ctx.enter_context(tc.psum_pool(name="transposed", bufs=4))
+        score_banks = ctx.enter_context(tc.psum_pool(name="scores", bufs=2))
         sums = ctx.enter_context(tc.psum_pool(name="sums", bufs=2))
 
         q_view = q_rot.rearrange("(i p) h d -> p i (h d)", p=P)
@@ -69,12 +70,12 @@ def tile_causalselfattention_pb_kernel(tc, x, Wv, vi, lamb, q_rot, k_rot, out):
         def starts_a_load(head):
             return 0 <= head < HEADS and head % HEADS_PER_LOAD == 0
 
-        first_step = -(LEAD + 2)
-        last_step = HEADS + 2
+        first_step = -(LEAD + 3)
+        last_step = HEADS + 1
         x_step = -2
 
         for step in range(first_step, last_step):
-            head = step + LEAD + 2
+            head = step + LEAD + 3
             if starts_a_load(head):
                 group = head // HEADS_PER_LOAD
                 cols = slice(group * LOAD_COLS, (group + 1) * LOAD_COLS)
@@ -173,7 +174,7 @@ def tile_causalselfattention_pb_kernel(tc, x, Wv, vi, lamb, q_rot, k_rot, out):
         w_grouped, w_codes, w_scales = {}, {}, {}
         qk_t = {}
         e_grouped, e_codes, e_scales = {}, {}, {}
-        row_sum, row_scale = {}, {}
+        scaled, shift, row_sum, row_scale = {}, {}, {}, {}
         residual, v_sum, v_codes, v_scales = {}, {}, {}, {}
         y_sum = {}
 
@@ -246,55 +247,55 @@ def tile_causalselfattention_pb_kernel(tc, x, Wv, vi, lamb, q_rot, k_rot, out):
             qk_t[head] = qk_pool.tile([P, 2, TOKENS], BF16, name="qk_t")
             nc.scalar.copy(out=qk_t[head][:], in_=bank[:])
 
-        def scores_and_exponentials(head):
-            even_bank = score_banks.tile([P, BANK], F32, name="even_bank", tag="scores")
-            bank_1 = score_banks.tile([P, BANK], F32, name="bank_1", tag="scores")
-            bank_3 = score_banks.tile([P, BANK], F32, name="bank_3", tag="scores")
-            score = {
-                0: even_bank[:, 3 * P : 4 * P],
-                2: even_bank[:, 0 : 3 * P],
-                1: bank_1[:, 0 : 2 * P],
-                3: bank_3[:, 0 : 4 * P],
-            }
-            for i in (0, 2, 1, 3):
-                keys = (i + 1) * P
-                nc.tensor.matmul(
-                    out=score[i],
-                    lhsT=qk_t[head][:, 0, i * P : (i + 1) * P],
-                    rhs=qk_t[head][:, 1, 0:keys],
-                    start=True,
-                    stop=False,
-                )
-                nc.tensor.matmul(
-                    out=score[i][:, keys - P : keys],
-                    lhsT=ident_bf16[:],
-                    rhs=future_mask[:],
-                    start=False,
-                    stop=True,
-                )
-            neg_max = rows.tile([P, TOKEN_TILES], F32, name="neg_max")
-            shift = rows.tile([P, TOKEN_TILES], F32, name="shift")
+        def scores_and_maxima(head):
+            shift[head] = rows.tile([P, TOKEN_TILES], F32, name="shift")
+            scaled[head] = {}
+            for tiles in ((0, 2), (1,), (3,)):
+                bank = score_banks.tile([P, BANK], F32, name="score_bank", tag="scores")
+                score = {}
+                first_col = 0
+                for i in tiles:
+                    keys = (i + 1) * P
+                    score[i] = bank[:, first_col : first_col + keys]
+                    first_col += keys
+                    nc.tensor.matmul(
+                        out=score[i],
+                        lhsT=qk_t[head][:, 0, i * P : (i + 1) * P],
+                        rhs=qk_t[head][:, 1, 0:keys],
+                        start=True,
+                        stop=False,
+                    )
+                    nc.tensor.matmul(
+                        out=score[i][:, keys - P : keys],
+                        lhsT=ident_bf16[:],
+                        rhs=future_mask[:],
+                        start=False,
+                        stop=True,
+                    )
+                for i in tiles:
+                    scaled[head][i] = scaled_pool.tile([P, (i + 1) * P], F32, name="scaled%d" % i)
+                    nc.vector.tensor_scalar(
+                        out=scaled[head][i][:],
+                        in0=score[i],
+                        scalar1=-SCALE,
+                        scalar2=None,
+                        op0=ALU.mult,
+                        op1=ALU.min,
+                        accum_out=shift[head][:, i : i + 1],
+                    )
+
+        def exponentials(head):
             row_sum[head] = rows.tile([P, TOKEN_TILES], F32, name="row_sum")
             e_rows = e_tiles[head % E_TILES][:].rearrange("p (i u) -> p i u", i=TOKEN_TILES)
-            for parity in range(2):
-                pair = (parity, parity + 2)
-                both = slice(parity, TOKEN_TILES, 2)
-                for i in pair:
-                    nc.vector.tensor_reduce(
-                        out=neg_max[:, i : i + 1], in_=score[i], axis=AXIS.X, op=ALU.max, negate=True
-                    )
-                nc.vector.tensor_scalar(
-                    out=shift[:, both], in0=neg_max[:, both], scalar1=SCALE, scalar2=None, op0=ALU.mult
+            for i in range(TOKEN_TILES):
+                nc.scalar.activation(
+                    out=e_rows[:, i, 0 : (i + 1) * P],
+                    in_=scaled[head][i][:],
+                    func=ACT.Exp,
+                    bias=shift[head][:, i : i + 1],
+                    scale=-1.0,
+                    accum_out=row_sum[head][:, i : i + 1],
                 )
-                for i in pair:
-                    nc.scalar.activation(
-                        out=e_rows[:, i, 0 : (i + 1) * P],
-                        in_=score[i],
-                        func=ACT.Exp,
-                        bias=shift[:, i : i + 1],
-                        scale=SCALE,
-                        accum_out=row_sum[head][:, i : i + 1],
-                    )
 
         def transpose_probabilities(head):
             e_words = e_tiles[head % E_TILES][:].bitcast(F32).rearrange("p (i w) -> p i w", i=TOKEN_TILES)
@@ -339,24 +340,26 @@ def tile_causalselfattention_pb_kernel(tc, x, Wv, vi, lamb, q_rot, k_rot, out):
                 quantise_activations()
             if live(step + 2):
                 transpose_weights(step + 2)
-            if live(step + LEAD + 2):
-                transpose_queries_keys(step + LEAD + 2)
+            if live(step + LEAD + 3):
+                transpose_queries_keys(step + LEAD + 3)
             if live(step + LEAD):
                 transpose_probabilities(step + LEAD)
+            if live(step + LEAD + 1):
+                exponentials(step + LEAD + 1)
             if live(step + 1):
                 scale_residual(step + 1)
             v_grouped = mix_values(step) if live(step) else None
-            if live(step - 2):
-                normalise_and_store(step - 2)
+            if live(step - 1):
+                normalise_and_store(step - 1)
             if live(step):
                 quantise_values(step, v_grouped)
             if live(step + 2):
                 quantise_weights(step + 2)
-            if live(step + LEAD + 1):
-                scores_and_exponentials(step + LEAD + 1)
+            if live(step + LEAD + 2):
+                scores_and_maxima(step + LEAD + 2)
             if live(step + LEAD):
                 quantise_probabilities(step + LEAD)
             if live(step + 1):
                 project_values(step + 1)
-            if live(step - 1):
-                attend(step - 1)
+            if live(step):
+                attend(step)

@@ -38,8 +38,6 @@ FLOPS = 2 * TOKENS * DIM * DIM + 2 * 2 * HEADS * TOKENS * TOKENS * HEAD_DIM
 def tile_causalselfattention_pb_kernel(tc, x, Wv, vi, lamb, q_rot, k_rot, out):
     nc = tc.nc
     with ExitStack() as ctx:
-        ctx.enter_context(tc.manual_schedule())
-
         consts = ctx.enter_context(tc.tile_pool(name="consts", bufs=1))
         inputs = ctx.enter_context(tc.tile_pool(name="inputs", bufs=1))
         x_mx = ctx.enter_context(tc.tile_pool(name="x_mx", bufs=1))

@@ -49,7 +49,8 @@ def tile_causalselfattention_pb_kernel(tc, x, Wv, vi, lamb, q_rot, k_rot, out):
         scaled_pool = ctx.enter_context(tc.tile_pool(name="scaled", bufs=2))
         rows = ctx.enter_context(tc.tile_pool(name="rows", bufs=LEAD + 5))
         work = ctx.enter_context(tc.tile_pool(name="work", bufs=3))
-        transposed = ctx.enter_context(tc.psum_pool(name="transposed", bufs=4))
+        transposed = ctx.enter_context(tc.psum_pool(name="transposed", bufs=3))
+        kept_bank = ctx.enter_context(tc.psum_pool(name="kept_bank", bufs=1))
         score_banks = ctx.enter_context(tc.psum_pool(name="scores", bufs=2))
         sums = ctx.enter_context(tc.psum_pool(name="sums", bufs=2))
 
@@ -129,24 +130,30 @@ def tile_causalselfattention_pb_kernel(tc, x, Wv, vi, lamb, q_rot, k_rot, out):
             out=one_minus_lam[:], in0=lam[:], scalar1=-1.0, scalar2=1.0, op0=ALU.mult, op1=ALU.add
         )
 
+        def transpose_words(bank, source_words, first_run, halves):
+            for run in range(2):
+                for half in halves:
+                    nc.tensor.transpose(
+                        bank[:, run, half, :],
+                        source_words[:, first_run + run, half * P : (half + 1) * P],
+                        ident_f32[:],
+                    )
+
+        def words_of(grouped):
+            return grouped[:].bitcast(F32).rearrange("p (run row half) -> p run row half", run=4, half=2)
+
+        def empty_bank(copy_out, bank, grouped, first_run):
+            copy_out(
+                out=words_of(grouped)[:, first_run : first_run + 2],
+                in_=bank[:].rearrange("p run half row -> p run row half"),
+            )
+
         def pairs_onto_partitions(source_words, name, copy_first, copy_second):
             grouped = grouped_pool.tile([P, PACK * BANK], BF16, name=name, tag="grouped", align_bytes=64)
-            grouped_words = grouped[:].bitcast(F32).rearrange(
-                "p (run row half) -> p run row half", run=4, half=2
-            )
-            for pair, copy_out in enumerate((copy_first, copy_second)):
+            for first_run, copy_out in ((0, copy_first), (2, copy_second)):
                 bank = transposed.tile([P, 2, 2, P], F32, name="word_bank", tag="transposed")
-                for run in range(2):
-                    for half in range(2):
-                        nc.tensor.transpose(
-                            bank[:, run, half, :],
-                            source_words[:, 2 * pair + run, half * P : (half + 1) * P],
-                            ident_f32[:],
-                        )
-                copy_out(
-                    out=grouped_words[:, 2 * pair : 2 * pair + 2],
-                    in_=bank[:].rearrange("p run half row -> p run row half"),
-                )
+                transpose_words(bank, source_words, first_run, (0, 1))
+                empty_bank(copy_out, bank, grouped, first_run)
             return grouped
 
         def quantise(grouped, codes, scales):
@@ -295,9 +302,21 @@ def tile_causalselfattention_pb_kernel(tc, x, Wv, vi, lamb, q_rot, k_rot, out):
                     accum_out=row_sum[head][:, i : i + 1],
                 )
 
+        def words_of_e(head):
+            return e_tiles[head % E_TILES][:].bitcast(F32).rearrange("p (i w) -> p i w", i=TOKEN_TILES)
+
+        low_bank = kept_bank.tile([P, 2, 2, P], F32, name="low_bank")
+        transpose_words(low_bank, words_of_e(0), 0, (1,))
+
         def transpose_probabilities(head):
-            e_words = e_tiles[head % E_TILES][:].bitcast(F32).rearrange("p (i w) -> p i w", i=TOKEN_TILES)
-            e_grouped[head] = pairs_onto_partitions(e_words, "e_grouped", nc.scalar.copy, nc.scalar.copy)
+            e_grouped[head] = grouped_pool.tile(
+                [P, PACK * BANK], BF16, name="e_grouped", tag="grouped", align_bytes=64
+            )
+            transpose_words(low_bank, words_of_e(head), 0, (0,))
+            empty_bank(nc.scalar.copy, low_bank, e_grouped[head], 0)
+            high_bank = transposed.tile([P, 2, 2, P], F32, name="high_bank", tag="transposed")
+            transpose_words(high_bank, words_of_e(head), 2, (0, 1))
+            empty_bank(nc.scalar.copy, high_bank, e_grouped[head], 2)
 
         def quantise_probabilities(head):
             e_codes[head] = e_mx.tile([P, TOKENS], U32, name="e_codes", align_bytes=64)

@@ -49,10 +49,7 @@ def tile_causalselfattention_pb_kernel(tc, x, Wv, vi, lamb, q_rot, k_rot, out):
         scaled_pool = ctx.enter_context(tc.tile_pool(name="scaled", bufs=2))
         rows = ctx.enter_context(tc.tile_pool(name="rows", bufs=LEAD + 5))
         work = ctx.enter_context(tc.tile_pool(name="work", bufs=3))
-        transposed = ctx.enter_context(tc.psum_pool(name="transposed", bufs=3))
-        kept_bank = ctx.enter_context(tc.psum_pool(name="kept_bank", bufs=1))
-        score_banks = ctx.enter_context(tc.psum_pool(name="scores", bufs=2))
-        sums = ctx.enter_context(tc.psum_pool(name="sums", bufs=2))
+        banks = ctx.enter_context(tc.psum_pool(name="banks", bufs=8))
 
         q_view = q_rot.rearrange("(i p) h d -> p i (h d)", p=P)
         k_view = k_rot.rearrange("(i p) h d -> p i (h d)", p=P)
@@ -130,30 +127,24 @@ def tile_causalselfattention_pb_kernel(tc, x, Wv, vi, lamb, q_rot, k_rot, out):
             out=one_minus_lam[:], in0=lam[:], scalar1=-1.0, scalar2=1.0, op0=ALU.mult, op1=ALU.add
         )
 
-        def transpose_words(bank, source_words, first_run, halves):
-            for run in range(2):
-                for half in halves:
-                    nc.tensor.transpose(
-                        bank[:, run, half, :],
-                        source_words[:, first_run + run, half * P : (half + 1) * P],
-                        ident_f32[:],
-                    )
-
-        def words_of(grouped):
-            return grouped[:].bitcast(F32).rearrange("p (run row half) -> p run row half", run=4, half=2)
-
-        def empty_bank(copy_out, bank, grouped, first_run):
-            copy_out(
-                out=words_of(grouped)[:, first_run : first_run + 2],
-                in_=bank[:].rearrange("p run half row -> p run row half"),
-            )
-
         def pairs_onto_partitions(source_words, name, copy_first, copy_second):
             grouped = grouped_pool.tile([P, PACK * BANK], BF16, name=name, tag="grouped", align_bytes=64)
-            for first_run, copy_out in ((0, copy_first), (2, copy_second)):
-                bank = transposed.tile([P, 2, 2, P], F32, name="word_bank", tag="transposed")
-                transpose_words(bank, source_words, first_run, (0, 1))
-                empty_bank(copy_out, bank, grouped, first_run)
+            grouped_words = grouped[:].bitcast(F32).rearrange(
+                "p (run row half) -> p run row half", run=4, half=2
+            )
+            for pair, copy_out in enumerate((copy_first, copy_second)):
+                bank = banks.tile([P, 2, 2, P], F32, name="word_bank", tag="bank")
+                for run in range(2):
+                    for half in range(2):
+                        nc.tensor.transpose(
+                            bank[:, run, half, :],
+                            source_words[:, 2 * pair + run, half * P : (half + 1) * P],
+                            ident_f32[:],
+                        )
+                copy_out(
+                    out=grouped_words[:, 2 * pair : 2 * pair + 2],
+                    in_=bank[:].rearrange("p run half row -> p run row half"),
+                )
             return grouped
 
         def quantise(grouped, codes, scales):
@@ -193,7 +184,7 @@ def tile_causalselfattention_pb_kernel(tc, x, Wv, vi, lamb, q_rot, k_rot, out):
             quantise(w_grouped[head], w_codes[head][:], w_scales[head][:])
 
         def project_values(head):
-            v_sum[head] = sums.tile([P, PACK, HEAD_DIM], F32, name="v_sum", tag="sums")
+            v_sum[head] = banks.tile([P, PACK, HEAD_DIM], F32, name="v_sum", tag="bank")
             for j in range(TOKEN_TILES):
                 for c in range(K_PASSES):
                     tokens = slice(j * P, (j + 1) * P)
@@ -245,7 +236,7 @@ def tile_causalselfattention_pb_kernel(tc, x, Wv, vi, lamb, q_rot, k_rot, out):
         def transpose_queries_keys(head):
             group = head // HEADS_PER_LOAD
             cols = slice((head % HEADS_PER_LOAD) * HEAD_DIM, (head % HEADS_PER_LOAD + 1) * HEAD_DIM)
-            bank = transposed.tile([P, 2, TOKENS], BF16, name="qk_bank", tag="transposed")
+            bank = banks.tile([P, 2, TOKENS], BF16, name="qk_bank", tag="bank")
             for which, raw in enumerate((q_raw[group], k_raw[group])):
                 for i in range(TOKEN_TILES):
                     nc.tensor.transpose(bank[:, which, i * P : (i + 1) * P], raw[:, i, cols], ident_bf16[:])
@@ -256,7 +247,7 @@ def tile_causalselfattention_pb_kernel(tc, x, Wv, vi, lamb, q_rot, k_rot, out):
             shift[head] = rows.tile([P, TOKEN_TILES], F32, name="shift")
             scaled[head] = {}
             for tiles in ((0, 2), (1,), (3,)):
-                bank = score_banks.tile([P, BANK], F32, name="score_bank", tag="scores")
+                bank = banks.tile([P, BANK], F32, name="score_bank", tag="bank")
                 score = {}
                 first_col = 0
                 for i in tiles:
@@ -302,21 +293,9 @@ def tile_causalselfattention_pb_kernel(tc, x, Wv, vi, lamb, q_rot, k_rot, out):
                     accum_out=row_sum[head][:, i : i + 1],
                 )
 
-        def words_of_e(head):
-            return e_tiles[head % E_TILES][:].bitcast(F32).rearrange("p (i w) -> p i w", i=TOKEN_TILES)
-
-        low_bank = kept_bank.tile([P, 2, 2, P], F32, name="low_bank")
-        transpose_words(low_bank, words_of_e(0), 0, (1,))
-
         def transpose_probabilities(head):
-            e_grouped[head] = grouped_pool.tile(
-                [P, PACK * BANK], BF16, name="e_grouped", tag="grouped", align_bytes=64
-            )
-            transpose_words(low_bank, words_of_e(head), 0, (0,))
-            empty_bank(nc.scalar.copy, low_bank, e_grouped[head], 0)
-            high_bank = transposed.tile([P, 2, 2, P], F32, name="high_bank", tag="transposed")
-            transpose_words(high_bank, words_of_e(head), 2, (0, 1))
-            empty_bank(nc.scalar.copy, high_bank, e_grouped[head], 2)
+            e_words = e_tiles[head % E_TILES][:].bitcast(F32).rearrange("p (i w) -> p i w", i=TOKEN_TILES)
+            e_grouped[head] = pairs_onto_partitions(e_words, "e_grouped", nc.scalar.copy, nc.scalar.copy)
 
         def quantise_probabilities(head):
             e_codes[head] = e_mx.tile([P, TOKENS], U32, name="e_codes", align_bytes=64)
@@ -326,7 +305,7 @@ def tile_causalselfattention_pb_kernel(tc, x, Wv, vi, lamb, q_rot, k_rot, out):
             nc.vector.reciprocal(out=row_scale[head][:], in_=row_sum[head][:])
 
         def attend(head):
-            y_sum[head] = sums.tile([P, TOKEN_TILES, HEAD_DIM], F32, name="y_sum", tag="sums")
+            y_sum[head] = banks.tile([P, TOKEN_TILES, HEAD_DIM], F32, name="y_sum", tag="bank")
             for i in range(TOKEN_TILES):
                 queries = slice(i * P, (i + 1) * P)
                 nc.tensor.matmul_mx(

@@ -49,7 +49,8 @@ def tile_causalselfattention_pb_kernel(tc, x, Wv, vi, lamb, q_rot, k_rot, out):
         scaled_pool = ctx.enter_context(tc.tile_pool(name="scaled", bufs=2))
         rows = ctx.enter_context(tc.tile_pool(name="rows", bufs=LEAD + 5))
         work = ctx.enter_context(tc.tile_pool(name="work", bufs=3))
-        banks = ctx.enter_context(tc.psum_pool(name="banks", bufs=8))
+        banks = ctx.enter_context(tc.psum_pool(name="banks", bufs=7))
+        kept_bank = ctx.enter_context(tc.psum_pool(name="kept_bank", bufs=1))
 
         q_view = q_rot.rearrange("(i p) h d -> p i (h d)", p=P)
         k_view = k_rot.rearrange("(i p) h d -> p i (h d)", p=P)
@@ -127,24 +128,30 @@ def tile_causalselfattention_pb_kernel(tc, x, Wv, vi, lamb, q_rot, k_rot, out):
             out=one_minus_lam[:], in0=lam[:], scalar1=-1.0, scalar2=1.0, op0=ALU.mult, op1=ALU.add
         )
 
+        def transpose_words(bank, source_words, first_run, halves):
+            for run in range(2):
+                for half in halves:
+                    nc.tensor.transpose(
+                        bank[:, run, half, :],
+                        source_words[:, first_run + run, half * P : (half + 1) * P],
+                        ident_f32[:],
+                    )
+
+        def words_of(grouped):
+            return grouped[:].bitcast(F32).rearrange("p (run row half) -> p run row half", run=4, half=2)
+
+        def empty_bank(copy_out, bank, grouped, first_run):
+            copy_out(
+                out=words_of(grouped)[:, first_run : first_run + 2],
+                in_=bank[:].rearrange("p run half row -> p run row half"),
+            )
+
         def pairs_onto_partitions(source_words, name, copy_first, copy_second):
             grouped = grouped_pool.tile([P, PACK * BANK], BF16, name=name, tag="grouped", align_bytes=64)
-            grouped_words = grouped[:].bitcast(F32).rearrange(
-                "p (run row half) -> p run row half", run=4, half=2
-            )
-            for pair, copy_out in enumerate((copy_first, copy_second)):
+            for first_run, copy_out in ((0, copy_first), (2, copy_second)):
                 bank = banks.tile([P, 2, 2, P], F32, name="word_bank", tag="bank")
-                for run in range(2):
-                    for half in range(2):
-                        nc.tensor.transpose(
-                            bank[:, run, half, :],
-                            source_words[:, 2 * pair + run, half * P : (half + 1) * P],
-                            ident_f32[:],
-                        )
-                copy_out(
-                    out=grouped_words[:, 2 * pair : 2 * pair + 2],
-                    in_=bank[:].rearrange("p run half row -> p run row half"),
-                )
+                transpose_words(bank, source_words, first_run, (0, 1))
+                empty_bank(copy_out, bank, grouped, first_run)
             return grouped
 
         def quantise(grouped, codes, scales):
@@ -293,9 +300,21 @@ def tile_causalselfattention_pb_kernel(tc, x, Wv, vi, lamb, q_rot, k_rot, out):
                     accum_out=row_sum[head][:, i : i + 1],
                 )
 
+        def words_of_e(head):
+            return e_tiles[head % E_TILES][:].bitcast(F32).rearrange("p (i w) -> p i w", i=TOKEN_TILES)
+
+        low_bank = kept_bank.tile([P, 2, 2, P], F32, name="low_bank")
+        transpose_words(low_bank, words_of_e(0), 0, (1,))
+
         def transpose_probabilities(head):
-            e_words = e_tiles[head % E_TILES][:].bitcast(F32).rearrange("p (i w) -> p i w", i=TOKEN_TILES)
-            e_grouped[head] = pairs_onto_partitions(e_words, "e_grouped", nc.scalar.copy, nc.scalar.copy)
+            e_grouped[head] = grouped_pool.tile(
+                [P, PACK * BANK], BF16, name="e_grouped", tag="grouped", align_bytes=64
+            )
+            transpose_words(low_bank, words_of_e(head), 0, (0,))
+            empty_bank(nc.scalar.copy, low_bank, e_grouped[head], 0)
+            high_bank = banks.tile([P, 2, 2, P], F32, name="high_bank", tag="bank")
+            transpose_words(high_bank, words_of_e(head), 2, (0, 1))
+            empty_bank(nc.scalar.copy, high_bank, e_grouped[head], 2)
 
         def quantise_probabilities(head):
             e_codes[head] = e_mx.tile([P, TOKENS], U32, name="e_codes", align_bytes=64)

@@ -41,16 +41,14 @@ def tile_causalselfattention_pb_kernel(tc, x, Wv, vi, lamb, q_rot, k_rot, out):
         consts = ctx.enter_context(tc.tile_pool(name="consts", bufs=1))
         inputs = ctx.enter_context(tc.tile_pool(name="inputs", bufs=1))
         x_mx = ctx.enter_context(tc.tile_pool(name="x_mx", bufs=1))
-        grouped_pool = ctx.enter_context(tc.tile_pool(name="grouped", bufs=4))
-        w_mx = ctx.enter_context(tc.tile_pool(name="w_mx", bufs=3))
-        e_mx = ctx.enter_context(tc.tile_pool(name="e_mx", bufs=LEAD + 3))
+        grouped_pool = ctx.enter_context(tc.tile_pool(name="grouped", bufs=3))
+        pair_mx = ctx.enter_context(tc.tile_pool(name="pair_mx", bufs=LEAD + 3))
         v_mx = ctx.enter_context(tc.tile_pool(name="v_mx", bufs=3))
         qk_pool = ctx.enter_context(tc.tile_pool(name="qk", bufs=3))
         scaled_pool = ctx.enter_context(tc.tile_pool(name="scaled", bufs=2))
         rows = ctx.enter_context(tc.tile_pool(name="rows", bufs=LEAD + 5))
         work = ctx.enter_context(tc.tile_pool(name="work", bufs=3))
-        banks = ctx.enter_context(tc.psum_pool(name="banks", bufs=7))
-        kept_bank = ctx.enter_context(tc.psum_pool(name="kept_bank", bufs=1))
+        banks = ctx.enter_context(tc.psum_pool(name="banks", bufs=8))
 
         q_view = q_rot.rearrange("(i p) h d -> p i (h d)", p=P)
         k_view = k_rot.rearrange("(i p) h d -> p i (h d)", p=P)
@@ -128,67 +126,72 @@ def tile_causalselfattention_pb_kernel(tc, x, Wv, vi, lamb, q_rot, k_rot, out):
             out=one_minus_lam[:], in0=lam[:], scalar1=-1.0, scalar2=1.0, op0=ALU.mult, op1=ALU.add
         )
 
-        def transpose_words(bank, source_words, first_run, halves):
-            for run in range(2):
-                for half in halves:
-                    nc.tensor.transpose(
-                        bank[:, run, half, :],
-                        source_words[:, first_run + run, half * P : (half + 1) * P],
-                        ident_f32[:],
-                    )
+        def new_grouped():
+            return grouped_pool.tile([P, 2, PACK * BANK], BF16, name="grouped", align_bytes=64)
 
-        def words_of(grouped):
-            return grouped[:].bitcast(F32).rearrange("p (run row half) -> p run row half", run=4, half=2)
-
-        def empty_bank(copy_out, bank, grouped, first_run):
-            copy_out(
-                out=words_of(grouped)[:, first_run : first_run + 2],
-                in_=bank[:].rearrange("p run half row -> p run row half"),
+        def pairs_onto_partitions(source_words, grouped):
+            grouped_words = grouped.bitcast(F32).rearrange(
+                "p (run row half) -> p run row half", run=4, half=2
             )
-
-        def pairs_onto_partitions(source_words, name, copy_first, copy_second):
-            grouped = grouped_pool.tile([P, PACK * BANK], BF16, name=name, tag="grouped", align_bytes=64)
-            for first_run, copy_out in ((0, copy_first), (2, copy_second)):
+            for pair in range(2):
                 bank = banks.tile([P, 2, 2, P], F32, name="word_bank", tag="bank")
-                transpose_words(bank, source_words, first_run, (0, 1))
-                empty_bank(copy_out, bank, grouped, first_run)
-            return grouped
+                for run in range(2):
+                    for half in range(2):
+                        nc.tensor.transpose(
+                            bank[:, run, half, :],
+                            source_words[:, 2 * pair + run, half * P : (half + 1) * P],
+                            ident_f32[:],
+                        )
+                nc.scalar.copy(
+                    out=grouped_words[:, 2 * pair : 2 * pair + 2],
+                    in_=bank[:].rearrange("p run half row -> p run row half"),
+                )
 
         def quantise(grouped, codes, scales):
-            nc.vector.quantize_mx(out=codes.bitcast(FP8X4), scales=scales, in_=grouped[:])
+            nc.vector.quantize_mx(out=codes.bitcast(FP8X4), scales=scales, in_=grouped)
 
         x_codes = x_mx.tile([P, K_PASSES, TOKENS], U32, name="x_codes", align_bytes=64)
         x_scales = x_mx.tile([P, K_PASSES, TOKENS], U8, name="x_scales", align_bytes=64)
 
         def quantise_activations():
             x_words = x_raw[:].bitcast(F32).rearrange("p (j w) -> p j w", j=TOKEN_TILES)
-            waiting = {}
-            for c in range(K_PASSES + 1):
-                if c < K_PASSES:
-                    waiting[c] = pairs_onto_partitions(
-                        x_words[:, :, c * WORDS : (c + 1) * WORDS],
-                        "x_grouped",
-                        nc.vector.tensor_copy,
-                        nc.scalar.copy,
-                    )
-                if c > 0:
-                    quantise(waiting[c - 1], x_codes[:, c - 1, :], x_scales[:, c - 1, :])
+            for first in range(0, K_PASSES, 2):
+                grouped = new_grouped()
+                for n in range(2):
+                    c = first + n
+                    pairs_onto_partitions(x_words[:, :, c * WORDS : (c + 1) * WORDS], grouped[:, n, :])
+                quantise(
+                    grouped[:].rearrange("p n w -> p (n w)"),
+                    x_codes[:, first : first + 2, :].rearrange("p c t -> p (c t)"),
+                    x_scales[:, first : first + 2, :].rearrange("p c t -> p (c t)"),
+                )
 
-        w_grouped, w_codes, w_scales = {}, {}, {}
+        w_codes, w_scales = {}, {}
         qk_t = {}
-        e_grouped, e_codes, e_scales = {}, {}, {}
+        e_codes, e_scales = {}, {}
         scaled, shift, row_sum, row_scale = {}, {}, {}, {}
         residual, v_sum, v_codes, v_scales = {}, {}, {}, {}
         y_sum = {}
 
-        def transpose_weights(head):
+        def transpose_weights(head, grouped):
             w_words = w_raw[head][:].bitcast(F32).rearrange("p (c w) -> p c w", c=K_PASSES)
-            w_grouped[head] = pairs_onto_partitions(w_words, "w_grouped", nc.scalar.copy, nc.scalar.copy)
+            pairs_onto_partitions(w_words, grouped)
 
-        def quantise_weights(head):
-            w_codes[head] = w_mx.tile([P, K_PASSES * HEAD_DIM], U32, name="w_codes", align_bytes=64)
-            w_scales[head] = w_mx.tile([P, K_PASSES * HEAD_DIM], U8, name="w_scales", align_bytes=64)
-            quantise(w_grouped[head], w_codes[head][:], w_scales[head][:])
+        def quantise_weights_and_probabilities(w_head, e_head, grouped):
+            codes = pair_mx.tile([P, 2, BANK], U32, name="pair_codes", align_bytes=64)
+            scales = pair_mx.tile([P, 2, BANK], U8, name="pair_scales", align_bytes=64)
+            first = 0 if live(w_head) else 1
+            last = 2 if live(e_head) else 1
+            quantise(
+                grouped[:, first:last, :].rearrange("p n w -> p (n w)"),
+                codes[:, first:last, :].rearrange("p n w -> p (n w)"),
+                scales[:, first:last, :].rearrange("p n w -> p (n w)"),
+            )
+            w_codes[w_head], w_scales[w_head] = codes[:, 0, :], scales[:, 0, :]
+            e_codes[e_head], e_scales[e_head] = codes[:, 1, :], scales[:, 1, :]
+            if live(e_head):
+                row_scale[e_head] = rows.tile([P, TOKEN_TILES], F32, name="row_scale")
+                nc.vector.reciprocal(out=row_scale[e_head][:], in_=row_sum[e_head][:])
 
         def project_values(head):
             v_sum[head] = banks.tile([P, PACK, HEAD_DIM], F32, name="v_sum", tag="bank")
@@ -300,28 +303,9 @@ def tile_causalselfattention_pb_kernel(tc, x, Wv, vi, lamb, q_rot, k_rot, out):
                     accum_out=row_sum[head][:, i : i + 1],
                 )
 
-        def words_of_e(head):
-            return e_tiles[head % E_TILES][:].bitcast(F32).rearrange("p (i w) -> p i w", i=TOKEN_TILES)
-
-        low_bank = kept_bank.tile([P, 2, 2, P], F32, name="low_bank")
-        transpose_words(low_bank, words_of_e(0), 0, (1,))
-
-        def transpose_probabilities(head):
-            e_grouped[head] = grouped_pool.tile(
-                [P, PACK * BANK], BF16, name="e_grouped", tag="grouped", align_bytes=64
-            )
-            transpose_words(low_bank, words_of_e(head), 0, (0,))
-            empty_bank(nc.scalar.copy, low_bank, e_grouped[head], 0)
-            high_bank = banks.tile([P, 2, 2, P], F32, name="high_bank", tag="bank")
-            transpose_words(high_bank, words_of_e(head), 2, (0, 1))
-            empty_bank(nc.scalar.copy, high_bank, e_grouped[head], 2)
-
-        def quantise_probabilities(head):
-            e_codes[head] = e_mx.tile([P, TOKENS], U32, name="e_codes", align_bytes=64)
-            e_scales[head] = e_mx.tile([P, TOKENS], U8, name="e_scales", align_bytes=64)
-            quantise(e_grouped[head], e_codes[head][:], e_scales[head][:])
-            row_scale[head] = rows.tile([P, TOKEN_TILES], F32, name="row_scale")
-            nc.vector.reciprocal(out=row_scale[head][:], in_=row_sum[head][:])
+        def transpose_probabilities(head, grouped):
+            e_words = e_tiles[head % E_TILES][:].bitcast(F32).rearrange("p (i w) -> p i w", i=TOKEN_TILES)
+            pairs_onto_partitions(e_words, grouped)
 
         def attend(head):
             y_sum[head] = banks.tile([P, TOKEN_TILES, HEAD_DIM], F32, name="y_sum", tag="bank")
@@ -353,12 +337,13 @@ def tile_causalselfattention_pb_kernel(tc, x, Wv, vi, lamb, q_rot, k_rot, out):
         for step in range(first_step, last_step):
             if step == x_step:
                 quantise_activations()
+            grouped = new_grouped() if live(step + 2) or live(step + LEAD) else None
             if live(step + 2):
-                transpose_weights(step + 2)
+                transpose_weights(step + 2, grouped[:, 0, :])
             if live(step + LEAD + 3):
                 transpose_queries_keys(step + LEAD + 3)
             if live(step + LEAD):
-                transpose_probabilities(step + LEAD)
+                transpose_probabilities(step + LEAD, grouped[:, 1, :])
             if live(step + LEAD + 1):
                 exponentials(step + LEAD + 1)
             if live(step + 1):
@@ -368,12 +353,10 @@ def tile_causalselfattention_pb_kernel(tc, x, Wv, vi, lamb, q_rot, k_rot, out):
                 normalise_and_store(step - 1)
             if live(step):
                 quantise_values(step, v_grouped)
-            if live(step + 2):
-                quantise_weights(step + 2)
             if live(step + LEAD + 2):
                 scores_and_maxima(step + LEAD + 2)
-            if live(step + LEAD):
-                quantise_probabilities(step + LEAD)
+            if live(step + 2) or live(step + LEAD):
+                quantise_weights_and_probabilities(step + 2, step + LEAD, grouped)
             if live(step + 1):
                 project_values(step + 1)
             if live(step):

@@ -11,6 +11,7 @@ FP8X4 = mybir.dt.float8_e4m3fn_x4
 ALU = mybir.AluOpType
 ACT = mybir.ActivationFunctionType
 AXIS = mybir.AxisListType
+ENGINE = mybir.EngineType
 
 P = 128
 PACK = 4
@@ -334,30 +335,31 @@ def tile_causalselfattention_pb_kernel(tc, x, Wv, vi, lamb, q_rot, k_rot, out):
         def live(head):
             return 0 <= head < HEADS
 
-        for step in range(first_step, last_step):
-            if step == x_step:
-                quantise_activations()
-            grouped = new_grouped() if live(step + 2) or live(step + LEAD) else None
-            if live(step + 2):
-                transpose_weights(step + 2, grouped[:, 0, :])
-            if live(step + LEAD + 3):
-                transpose_queries_keys(step + LEAD + 3)
-            if live(step + LEAD):
-                transpose_probabilities(step + LEAD, grouped[:, 1, :])
-            if live(step + LEAD + 1):
-                exponentials(step + LEAD + 1)
-            if live(step + 1):
-                scale_residual(step + 1)
-            v_grouped = mix_values(step) if live(step) else None
-            if live(step - 1):
-                normalise_and_store(step - 1)
-            if live(step):
-                quantise_values(step, v_grouped)
-            if live(step + LEAD + 2):
-                scores_and_maxima(step + LEAD + 2)
-            if live(step + 2) or live(step + LEAD):
-                quantise_weights_and_probabilities(step + 2, step + LEAD, grouped)
-            if live(step + 1):
-                project_values(step + 1)
-            if live(step):
-                attend(step)
+        with tc.manual_schedule(engines={ENGINE.PE, ENGINE.Activation, ENGINE.DVE}):
+            for step in range(first_step, last_step):
+                if step == x_step:
+                    quantise_activations()
+                grouped = new_grouped() if live(step + 2) or live(step + LEAD) else None
+                if live(step + 2):
+                    transpose_weights(step + 2, grouped[:, 0, :])
+                if live(step + LEAD + 3):
+                    transpose_queries_keys(step + LEAD + 3)
+                if live(step + LEAD):
+                    transpose_probabilities(step + LEAD, grouped[:, 1, :])
+                if live(step + LEAD + 1):
+                    exponentials(step + LEAD + 1)
+                if live(step + 1):
+                    scale_residual(step + 1)
+                v_grouped = mix_values(step) if live(step) else None
+                if live(step - 1):
+                    normalise_and_store(step - 1)
+                if live(step):
+                    quantise_values(step, v_grouped)
+                if live(step + LEAD + 2):
+                    scores_and_maxima(step + LEAD + 2)
+                if live(step + 2) or live(step + LEAD):
+                    quantise_weights_and_probabilities(step + 2, step + LEAD, grouped)
+                if live(step + 1):
+                    project_values(step + 1)
+                if live(step):
+                    attend(step)

@@ -23,6 +23,7 @@ HEAD_DIM = 128
 TOKEN_TILES = TOKENS // P
 K_PASSES = DIM // K_PASS
 WORDS = K_PASS // 2
+PSUM_BANKS = 8
 BANK = 512
 SCALE = HEAD_DIM ** -0.5
 MASKED = -1.0e30
@@ -30,7 +31,7 @@ MASKED = -1.0e30
 HEADS_PER_LOAD = 4
 LOAD_COLS = HEADS_PER_LOAD * HEAD_DIM
 
-LEAD = 1
+LEAD = 2
 E_TILES = 3
 
 FLOPS = 2 * TOKENS * DIM * DIM + 2 * 2 * HEADS * TOKENS * TOKENS * HEAD_DIM
@@ -49,7 +50,14 @@ def tile_causalselfattention_pb_kernel(tc, x, Wv, vi, lamb, q_rot, k_rot, out):
         scaled_pool = ctx.enter_context(tc.tile_pool(name="scaled", bufs=2))
         rows = ctx.enter_context(tc.tile_pool(name="rows", bufs=LEAD + 5))
         work = ctx.enter_context(tc.tile_pool(name="work", bufs=3))
-        banks = ctx.enter_context(tc.psum_pool(name="banks", bufs=8))
+        mix_pool = ctx.enter_context(tc.tile_pool(name="mix", bufs=5))
+        banks = ctx.enter_context(tc.psum_pool(name="banks", bufs=1))
+        banks_taken = []
+
+        def new_bank(shape, dtype):
+            turn = "bank%d" % (len(banks_taken) % PSUM_BANKS)
+            banks_taken.append(turn)
+            return banks.tile(shape, dtype, name=turn, tag=turn)
 
         q_view = q_rot.rearrange("(i p) h d -> p i (h d)", p=P)
         k_view = k_rot.rearrange("(i p) h d -> p i (h d)", p=P)
@@ -130,23 +138,25 @@ def tile_causalselfattention_pb_kernel(tc, x, Wv, vi, lamb, q_rot, k_rot, out):
         def new_grouped():
             return grouped_pool.tile([P, 2, PACK * BANK], BF16, name="grouped", align_bytes=64)
 
-        def pairs_onto_partitions(source_words, grouped):
+        def transpose_words(source_words, pair):
+            bank = new_bank([P, 2, 2, P], F32)
+            for run in range(2):
+                for half in range(2):
+                    nc.tensor.transpose(
+                        bank[:, run, half, :],
+                        source_words[:, 2 * pair + run, half * P : (half + 1) * P],
+                        ident_f32[:],
+                    )
+            return bank
+
+        def copy_words(bank, grouped, pair, copy=nc.scalar.copy):
             grouped_words = grouped.bitcast(F32).rearrange(
                 "p (run row half) -> p run row half", run=4, half=2
             )
-            for pair in range(2):
-                bank = banks.tile([P, 2, 2, P], F32, name="word_bank", tag="bank")
-                for run in range(2):
-                    for half in range(2):
-                        nc.tensor.transpose(
-                            bank[:, run, half, :],
-                            source_words[:, 2 * pair + run, half * P : (half + 1) * P],
-                            ident_f32[:],
-                        )
-                nc.scalar.copy(
-                    out=grouped_words[:, 2 * pair : 2 * pair + 2],
-                    in_=bank[:].rearrange("p run half row -> p run row half"),
-                )
+            copy(
+                out=grouped_words[:, 2 * pair : 2 * pair + 2],
+                in_=bank[:].rearrange("p run half row -> p run row half"),
+            )
 
         def quantise(grouped, codes, scales):
             nc.vector.quantize_mx(out=codes.bitcast(FP8X4), scales=scales, in_=grouped)
@@ -160,7 +170,9 @@ def tile_causalselfattention_pb_kernel(tc, x, Wv, vi, lamb, q_rot, k_rot, out):
                 grouped = new_grouped()
                 for n in range(2):
                     c = first + n
-                    pairs_onto_partitions(x_words[:, :, c * WORDS : (c + 1) * WORDS], grouped[:, n, :])
+                    for pair in range(2):
+                        bank = transpose_words(x_words[:, :, c * WORDS : (c + 1) * WORDS], pair)
+                        copy_words(bank, grouped[:, n, :], pair, (nc.scalar.copy, nc.vector.tensor_copy)[pair])
                 quantise(
                     grouped[:].rearrange("p n w -> p (n w)"),
                     x_codes[:, first : first + 2, :].rearrange("p c t -> p (c t)"),
@@ -174,9 +186,9 @@ def tile_causalselfattention_pb_kernel(tc, x, Wv, vi, lamb, q_rot, k_rot, out):
         residual, v_sum, v_codes, v_scales = {}, {}, {}, {}
         y_sum = {}
 
-        def transpose_weights(head, grouped):
+        def transpose_weights(head):
             w_words = w_raw[head][:].bitcast(F32).rearrange("p (c w) -> p c w", c=K_PASSES)
-            pairs_onto_partitions(w_words, grouped)
+            return [transpose_words(w_words, pair) for pair in range(2)]
 
         def quantise_weights_and_probabilities(w_head, e_head, grouped):
             codes = pair_mx.tile([P, 2, BANK], U32, name="pair_codes", align_bytes=64)
@@ -195,7 +207,7 @@ def tile_causalselfattention_pb_kernel(tc, x, Wv, vi, lamb, q_rot, k_rot, out):
                 nc.vector.reciprocal(out=row_scale[e_head][:], in_=row_sum[e_head][:])
 
         def project_values(head):
-            v_sum[head] = banks.tile([P, PACK, HEAD_DIM], F32, name="v_sum", tag="bank")
+            v_sum[head] = new_bank([P, PACK, HEAD_DIM], F32)
             for j in range(TOKEN_TILES):
                 for c in range(K_PASSES):
                     tokens = slice(j * P, (j + 1) * P)
@@ -213,7 +225,9 @@ def tile_causalselfattention_pb_kernel(tc, x, Wv, vi, lamb, q_rot, k_rot, out):
         def scale_residual(head):
             group = head // HEADS_PER_LOAD
             cols = slice((head % HEADS_PER_LOAD) * HEAD_DIM, (head % HEADS_PER_LOAD + 1) * HEAD_DIM)
-            residual[head] = work.tile([P, HEAD_DIM, PACK], F32, name="residual")
+            residual[head] = mix_pool.tile(
+                [P, HEAD_DIM, PACK], F32, name="residual", tag="mix", align_bytes=64
+            )
             nc.gpsimd.tensor_scalar(
                 out=residual[head][:],
                 in0=vi_raw[group][:, :, cols].rearrange("p j d -> p d j"),
@@ -224,7 +238,9 @@ def tile_causalselfattention_pb_kernel(tc, x, Wv, vi, lamb, q_rot, k_rot, out):
             )
 
         def mix_values(head):
-            v_grouped = work.tile([P, HEAD_DIM, PACK], BF16, name="v_grouped", align_bytes=64)
+            v_grouped = mix_pool.tile(
+                [P, HEAD_DIM, PACK], BF16, name="v_grouped", tag="mix", align_bytes=64
+            )
             nc.vector.scalar_tensor_tensor(
                 out=v_grouped[:],
                 in0=v_sum[head][:].rearrange("p j d -> p d j"),
@@ -247,54 +263,62 @@ def tile_causalselfattention_pb_kernel(tc, x, Wv, vi, lamb, q_rot, k_rot, out):
         def transpose_queries_keys(head):
             group = head // HEADS_PER_LOAD
             cols = slice((head % HEADS_PER_LOAD) * HEAD_DIM, (head % HEADS_PER_LOAD + 1) * HEAD_DIM)
-            bank = banks.tile([P, 2, TOKENS], BF16, name="qk_bank", tag="bank")
+            bank = new_bank([P, 2, TOKENS], BF16)
             for which, raw in enumerate((q_raw[group], k_raw[group])):
                 for i in range(TOKEN_TILES):
                     nc.tensor.transpose(bank[:, which, i * P : (i + 1) * P], raw[:, i, cols], ident_bf16[:])
+            return bank
+
+        def copy_queries_keys(head, bank):
             qk_t[head] = qk_pool.tile([P, 2, TOKENS], BF16, name="qk_t")
             nc.scalar.copy(out=qk_t[head][:], in_=bank[:])
 
-        def scores_and_maxima(head):
-            shift[head] = rows.tile([P, TOKEN_TILES], F32, name="shift")
-            scaled[head] = {}
-            for tiles in ((0, 2), (1,), (3,)):
-                bank = banks.tile([P, BANK], F32, name="score_bank", tag="bank")
-                score = {}
+        score = {}
+
+        def scores(head, tile_groups):
+            for tiles in tile_groups:
+                bank = new_bank([P, BANK], F32)
                 first_col = 0
                 for i in tiles:
                     keys = (i + 1) * P
-                    score[i] = bank[:, first_col : first_col + keys]
+                    score[head, i] = bank[:, first_col : first_col + keys]
                     first_col += keys
                     nc.tensor.matmul(
-                        out=score[i],
+                        out=score[head, i],
                         lhsT=qk_t[head][:, 0, i * P : (i + 1) * P],
                         rhs=qk_t[head][:, 1, 0:keys],
                         start=True,
                         stop=False,
                     )
                     nc.tensor.matmul(
-                        out=score[i][:, keys - P : keys],
+                        out=score[head, i][:, keys - P : keys],
                         lhsT=ident_bf16[:],
                         rhs=future_mask[:],
                         start=False,
                         stop=True,
                     )
-                for i in tiles:
-                    scaled[head][i] = scaled_pool.tile([P, (i + 1) * P], F32, name="scaled%d" % i)
-                    nc.vector.tensor_scalar(
-                        out=scaled[head][i][:],
-                        in0=score[i],
-                        scalar1=-SCALE,
-                        scalar2=None,
-                        op0=ALU.mult,
-                        op1=ALU.min,
-                        accum_out=shift[head][:, i : i + 1],
-                    )
 
-        def exponentials(head):
-            row_sum[head] = rows.tile([P, TOKEN_TILES], F32, name="row_sum")
+        def maxima(head, tiles):
+            if head not in shift:
+                shift[head] = rows.tile([P, TOKEN_TILES], F32, name="shift")
+                scaled[head] = {}
+            for i in tiles:
+                scaled[head][i] = scaled_pool.tile([P, (i + 1) * P], F32, name="scaled%d" % i)
+                nc.vector.tensor_scalar(
+                    out=scaled[head][i][:],
+                    in0=score[head, i],
+                    scalar1=-SCALE,
+                    scalar2=None,
+                    op0=ALU.mult,
+                    op1=ALU.min,
+                    accum_out=shift[head][:, i : i + 1],
+                )
+
+        def exponentials(head, tiles):
+            if head not in row_sum:
+                row_sum[head] = rows.tile([P, TOKEN_TILES], F32, name="row_sum")
             e_rows = e_tiles[head % E_TILES][:].rearrange("p (i u) -> p i u", i=TOKEN_TILES)
-            for i in range(TOKEN_TILES):
+            for i in tiles:
                 nc.scalar.activation(
                     out=e_rows[:, i, 0 : (i + 1) * P],
                     in_=scaled[head][i][:],
@@ -304,12 +328,12 @@ def tile_causalselfattention_pb_kernel(tc, x, Wv, vi, lamb, q_rot, k_rot, out):
                     accum_out=row_sum[head][:, i : i + 1],
                 )
 
-        def transpose_probabilities(head, grouped):
+        def transpose_probabilities(head):
             e_words = e_tiles[head % E_TILES][:].bitcast(F32).rearrange("p (i w) -> p i w", i=TOKEN_TILES)
-            pairs_onto_partitions(e_words, grouped)
+            return [transpose_words(e_words, pair) for pair in range(2)]
 
         def attend(head):
-            y_sum[head] = banks.tile([P, TOKEN_TILES, HEAD_DIM], F32, name="y_sum", tag="bank")
+            y_sum[head] = new_bank([P, TOKEN_TILES, HEAD_DIM], F32)
             for i in range(TOKEN_TILES):
                 queries = slice(i * P, (i + 1) * P)
                 nc.tensor.matmul_mx(
@@ -337,17 +361,22 @@ def tile_causalselfattention_pb_kernel(tc, x, Wv, vi, lamb, q_rot, k_rot, out):
 
         with tc.manual_schedule(engines={ENGINE.PE, ENGINE.Activation, ENGINE.DVE}):
             for step in range(first_step, last_step):
+                w_head, e_head, exp_head, score_head, qk_head = step + 2, step + LEAD, step + LEAD + 1, step + LEAD + 2, step + LEAD + 3
                 if step == x_step:
                     quantise_activations()
-                grouped = new_grouped() if live(step + 2) or live(step + LEAD) else None
-                if live(step + 2):
-                    transpose_weights(step + 2, grouped[:, 0, :])
-                if live(step + LEAD + 3):
-                    transpose_queries_keys(step + LEAD + 3)
-                if live(step + LEAD):
-                    transpose_probabilities(step + LEAD, grouped[:, 1, :])
-                if live(step + LEAD + 1):
-                    exponentials(step + LEAD + 1)
+                grouped = new_grouped() if live(w_head) or live(e_head) else None
+                if live(w_head):
+                    w_banks = transpose_weights(w_head)
+                    for pair in range(2):
+                        copy_words(w_banks[pair], grouped[:, 0, :], pair)
+                if live(qk_head):
+                    copy_queries_keys(qk_head, transpose_queries_keys(qk_head))
+                if live(e_head):
+                    e_banks = transpose_probabilities(e_head)
+                    for pair in range(2):
+                        copy_words(e_banks[pair], grouped[:, 1, :], pair)
+                if live(exp_head):
+                    exponentials(exp_head, (0, 1, 2, 3))
                 if live(step + 1):
                     scale_residual(step + 1)
                 v_grouped = mix_values(step) if live(step) else None
@@ -355,10 +384,11 @@ def tile_causalselfattention_pb_kernel(tc, x, Wv, vi, lamb, q_rot, k_rot, out):
                     normalise_and_store(step - 1)
                 if live(step):
                     quantise_values(step, v_grouped)
-                if live(step + LEAD + 2):
-                    scores_and_maxima(step + LEAD + 2)
-                if live(step + 2) or live(step + LEAD):
-                    quantise_weights_and_probabilities(step + 2, step + LEAD, grouped)
+                if live(score_head):
+                    scores(score_head, ((0, 2), (1,), (3,)))
+                    maxima(score_head, (0, 2, 1, 3))
+                if live(w_head) or live(e_head):
+                    quantise_weights_and_probabilities(w_head, e_head, grouped)
                 if live(step + 1):
                     project_values(step + 1)
                 if live(step):

@@ -49,7 +49,8 @@ def tile_causalselfattention_pb_kernel(tc, x, Wv, vi, lamb, q_rot, k_rot, out):
         qk_pool = ctx.enter_context(tc.tile_pool(name="qk", bufs=3))
         scaled_pool = ctx.enter_context(tc.tile_pool(name="scaled", bufs=2))
         rows = ctx.enter_context(tc.tile_pool(name="rows", bufs=LEAD + 5))
-        work = ctx.enter_context(tc.tile_pool(name="work", bufs=3))
+        y_pool = ctx.enter_context(tc.tile_pool(name="y", bufs=HEADS))
+        w_pool = ctx.enter_context(tc.tile_pool(name="w_raw", bufs=HEADS // 2))
         mix_pool = ctx.enter_context(tc.tile_pool(name="mix", bufs=5))
         banks = ctx.enter_context(tc.psum_pool(name="banks", bufs=1))
         banks_taken = []
@@ -93,7 +94,7 @@ def tile_causalselfattention_pb_kernel(tc, x, Wv, vi, lamb, q_rot, k_rot, out):
                     nc.sync.dma_start(out=x_halves[:, half, :], in_=x_view[:, half, :])
             head = step + 2
             if 0 <= head < HEADS:
-                w_raw[head] = inputs.tile([P, DIM], BF16, name="w_raw%d" % head)
+                w_raw[head] = w_pool.tile([P, DIM], BF16, name="w_raw")
                 nc.sync.dma_start(out=w_raw[head][:], in_=Wv[head * P : (head + 1) * P, :])
             head = step + 1
             if starts_a_load(head):
@@ -347,7 +348,7 @@ def tile_causalselfattention_pb_kernel(tc, x, Wv, vi, lamb, q_rot, k_rot, out):
                 )
 
         def normalise_and_store(head):
-            y = work.tile([P, TOKEN_TILES, HEAD_DIM], F32, name="y")
+            y = y_pool.tile([P, TOKEN_TILES, HEAD_DIM], F32, name="y")
             nc.vector.tensor_tensor(
                 out=y[:],
                 in0=y_sum[head][:],

@@ -24,6 +24,7 @@ TOKEN_TILES = TOKENS // P
 K_PASSES = DIM // K_PASS
 WORDS = K_PASS // 2
 PSUM_BANKS = 8
+MIX_BUFFERS = 5
 BANK = 512
 SCALE = HEAD_DIM ** -0.5
 MASKED = -1.0e30
@@ -51,7 +52,14 @@ def tile_causalselfattention_pb_kernel(tc, x, Wv, vi, lamb, q_rot, k_rot, out):
         rows = ctx.enter_context(tc.tile_pool(name="rows", bufs=LEAD + 5))
         y_pool = ctx.enter_context(tc.tile_pool(name="y", bufs=HEADS))
         w_pool = ctx.enter_context(tc.tile_pool(name="w_raw", bufs=HEADS // 2))
-        mix_pool = ctx.enter_context(tc.tile_pool(name="mix", bufs=5))
+        mix_pool = ctx.enter_context(tc.tile_pool(name="mix", bufs=1))
+        mix_taken = []
+
+        def new_mix_buffer(dtype):
+            turn = "mix%d" % (len(mix_taken) % MIX_BUFFERS)
+            mix_taken.append(turn)
+            return mix_pool.tile([P, HEAD_DIM, PACK], dtype, name=turn, tag=turn, align_bytes=64)
+
         banks = ctx.enter_context(tc.psum_pool(name="banks", bufs=1))
         banks_taken = []
 
@@ -226,9 +234,7 @@ def tile_causalselfattention_pb_kernel(tc, x, Wv, vi, lamb, q_rot, k_rot, out):
         def scale_residual(head):
             group = head // HEADS_PER_LOAD
             cols = slice((head % HEADS_PER_LOAD) * HEAD_DIM, (head % HEADS_PER_LOAD + 1) * HEAD_DIM)
-            residual[head] = mix_pool.tile(
-                [P, HEAD_DIM, PACK], F32, name="residual", tag="mix", align_bytes=64
-            )
+            residual[head] = new_mix_buffer(F32)
             nc.gpsimd.tensor_scalar(
                 out=residual[head][:],
                 in0=vi_raw[group][:, :, cols].rearrange("p j d -> p d j"),
@@ -239,9 +245,7 @@ def tile_causalselfattention_pb_kernel(tc, x, Wv, vi, lamb, q_rot, k_rot, out):
             )
 
         def mix_values(head):
-            v_grouped = mix_pool.tile(
-                [P, HEAD_DIM, PACK], BF16, name="v_grouped", tag="mix", align_bytes=64
-            )
+            v_grouped = new_mix_buffer(BF16)
             nc.vector.scalar_tensor_tensor(
                 out=v_grouped[:],
                 in0=v_sum[head][:].rearrange("p j d -> p d j"),

@@ -23,7 +23,7 @@ HEAD_DIM = 128
 TOKEN_TILES = TOKENS // P
 K_PASSES = DIM // K_PASS
 WORDS = K_PASS // 2
-PSUM_BANKS = 8
+TURNING_BANKS = 7
 MIX_BUFFERS = 5
 BANK = 512
 SCALE = HEAD_DIM ** -0.5
@@ -32,7 +32,7 @@ MASKED = -1.0e30
 HEADS_PER_LOAD = 4
 LOAD_COLS = HEADS_PER_LOAD * HEAD_DIM
 
-LEAD = 2
+LEAD = 1
 E_TILES = 3
 
 FLOPS = 2 * TOKENS * DIM * DIM + 2 * 2 * HEADS * TOKENS * TOKENS * HEAD_DIM
@@ -61,10 +61,11 @@ def tile_causalselfattention_pb_kernel(tc, x, Wv, vi, lamb, q_rot, k_rot, out):
             return mix_pool.tile([P, HEAD_DIM, PACK], dtype, name=turn, tag=turn, align_bytes=64)
 
         banks = ctx.enter_context(tc.psum_pool(name="banks", bufs=1))
+        kept_bank = banks.tile([P, 2, 2, P], F32, name="kept_bank", tag="kept_bank")
         banks_taken = []
 
         def new_bank(shape, dtype):
-            turn = "bank%d" % (len(banks_taken) % PSUM_BANKS)
+            turn = "bank%d" % (len(banks_taken) % TURNING_BANKS)
             banks_taken.append(turn)
             return banks.tile(shape, dtype, name=turn, tag=turn)
 
@@ -147,10 +148,9 @@ def tile_causalselfattention_pb_kernel(tc, x, Wv, vi, lamb, q_rot, k_rot, out):
         def new_grouped():
             return grouped_pool.tile([P, 2, PACK * BANK], BF16, name="grouped", align_bytes=64)
 
-        def transpose_words(source_words, pair):
-            bank = new_bank([P, 2, 2, P], F32)
+        def transpose_words(source_words, pair, bank, halves=(0, 1)):
             for run in range(2):
-                for half in range(2):
+                for half in halves:
                     nc.tensor.transpose(
                         bank[:, run, half, :],
                         source_words[:, 2 * pair + run, half * P : (half + 1) * P],
@@ -175,18 +175,22 @@ def tile_causalselfattention_pb_kernel(tc, x, Wv, vi, lamb, q_rot, k_rot, out):
 
         def quantise_activations():
             x_words = x_raw[:].bitcast(F32).rearrange("p (j w) -> p j w", j=TOKEN_TILES)
-            for first in range(0, K_PASSES, 2):
-                grouped = new_grouped()
-                for n in range(2):
-                    c = first + n
-                    for pair in range(2):
-                        bank = transpose_words(x_words[:, :, c * WORDS : (c + 1) * WORDS], pair)
-                        copy_words(bank, grouped[:, n, :], pair, (nc.scalar.copy, nc.vector.tensor_copy)[pair])
+            grouped = [new_grouped() for first in range(0, K_PASSES, 2)]
+            for half in range(2):
+                for c in range(K_PASSES):
+                    bank = new_bank([P, 2, 2, P], F32)
+                    transpose_words(x_words[:, :, c * WORDS : (c + 1) * WORDS], half, bank)
+                    copy = (nc.scalar.copy, nc.vector.tensor_copy)[c % 2]
+                    copy_words(bank, grouped[c // 2][:, c % 2, :], half, copy)
+            for n, first in enumerate(range(0, K_PASSES, 2)):
                 quantise(
-                    grouped[:].rearrange("p n w -> p (n w)"),
+                    grouped[n][:].rearrange("p n w -> p (n w)"),
                     x_codes[:, first : first + 2, :].rearrange("p c t -> p (c t)"),
                     x_scales[:, first : first + 2, :].rearrange("p c t -> p (c t)"),
                 )
+
+        zero_words = e_tiles[0][:].bitcast(F32).rearrange("p (i w) -> p i w", i=TOKEN_TILES)
+        transpose_words(zero_words, 0, kept_bank, halves=(1,))
 
         w_codes, w_scales = {}, {}
         qk_t = {}
@@ -197,7 +201,7 @@ def tile_causalselfattention_pb_kernel(tc, x, Wv, vi, lamb, q_rot, k_rot, out):
 
         def transpose_weights(head):
             w_words = w_raw[head][:].bitcast(F32).rearrange("p (c w) -> p c w", c=K_PASSES)
-            return [transpose_words(w_words, pair) for pair in range(2)]
+            return [transpose_words(w_words, pair, new_bank([P, 2, 2, P], F32)) for pair in range(2)]
 
         def quantise_weights_and_probabilities(w_head, e_head, grouped):
             codes = pair_mx.tile([P, 2, BANK], U32, name="pair_codes", align_bytes=64)
@@ -335,7 +339,10 @@ def tile_causalselfattention_pb_kernel(tc, x, Wv, vi, lamb, q_rot, k_rot, out):
 
         def transpose_probabilities(head):
             e_words = e_tiles[head % E_TILES][:].bitcast(F32).rearrange("p (i w) -> p i w", i=TOKEN_TILES)
-            return [transpose_words(e_words, pair) for pair in range(2)]
+            return [
+                transpose_words(e_words, 0, kept_bank, halves=(0,)),
+                transpose_words(e_words, 1, new_bank([P, 2, 2, P], F32)),
+            ]
 
         def attend(head):
             y_sum[head] = new_bank([P, TOKEN_TILES, HEAD_DIM], F32)

@@ -32,7 +32,7 @@ MASKED = -1.0e30
 HEADS_PER_LOAD = 4
 LOAD_COLS = HEADS_PER_LOAD * HEAD_DIM
 
-LEAD = 1
+LEAD = 2
 E_TILES = 3
 
 FLOPS = 2 * TOKENS * DIM * DIM + 2 * 2 * HEADS * TOKENS * TOKENS * HEAD_DIM
@@ -383,10 +383,14 @@ def tile_causalselfattention_pb_kernel(tc, x, Wv, vi, lamb, q_rot, k_rot, out):
                         copy_words(w_banks[pair], grouped[:, 0, :], pair)
                 if live(qk_head):
                     copy_queries_keys(qk_head, transpose_queries_keys(qk_head))
+                if live(score_head):
+                    scores(score_head, ((0, 2), (1,)))
                 if live(e_head):
                     e_banks = transpose_probabilities(e_head)
                     for pair in range(2):
                         copy_words(e_banks[pair], grouped[:, 1, :], pair)
+                if live(score_head):
+                    scores(score_head, ((3,),))
                 if live(exp_head):
                     exponentials(exp_head, (0, 1, 2, 3))
                 if live(step + 1):
@@ -397,7 +401,6 @@ def tile_causalselfattention_pb_kernel(tc, x, Wv, vi, lamb, q_rot, k_rot, out):
                 if live(step):
                     quantise_values(step, v_grouped)
                 if live(score_head):
-                    scores(score_head, ((0, 2), (1,), (3,)))
                     maxima(score_head, (0, 2, 1, 3))
                 if live(w_head) or live(e_head):
                     quantise_weights_and_probabilities(w_head, e_head, grouped)

@@ -32,7 +32,7 @@ MASKED = -1.0e30
 HEADS_PER_LOAD = 4
 LOAD_COLS = HEADS_PER_LOAD * HEAD_DIM
 
-LEAD = 2
+LEAD = 1
 E_TILES = 3
 
 FLOPS = 2 * TOKENS * DIM * DIM + 2 * 2 * HEADS * TOKENS * TOKENS * HEAD_DIM
@@ -358,21 +358,25 @@ def tile_causalselfattention_pb_kernel(tc, x, Wv, vi, lamb, q_rot, k_rot, out):
                     stop=True,
                 )
 
-        def normalise_and_store(head):
+        def normalise_and_store(head, parts=1):
             y = y_pool.tile([P, TOKEN_TILES, HEAD_DIM], F32, name="y")
-            nc.vector.tensor_tensor(
-                out=y[:],
-                in0=y_sum[head][:],
-                in1=row_scale[head][:].unsqueeze(2).to_broadcast([P, TOKEN_TILES, HEAD_DIM]),
-                op=ALU.mult,
-            )
-            nc.sync.dma_start(out=out_view[:, :, head, :], in_=y[:])
+            count = TOKEN_TILES // parts
+            for first in range(0, TOKEN_TILES, count):
+                tiles = slice(first, first + count)
+                nc.vector.tensor_tensor(
+                    out=y[:, tiles, :],
+                    in0=y_sum[head][:, tiles, :],
+                    in1=row_scale[head][:, tiles].unsqueeze(2).to_broadcast([P, count, HEAD_DIM]),
+                    op=ALU.mult,
+                )
+                nc.sync.dma_start(out=out_view[:, tiles, head, :], in_=y[:, tiles, :])
 
         def live(head):
             return 0 <= head < HEADS
 
         with tc.manual_schedule(engines={ENGINE.PE, ENGINE.Activation, ENGINE.DVE}):
-            for step in range(first_step, last_step):
+            last = HEADS - 1
+            for step in range(first_step, last - 1):
                 w_head, e_head, exp_head, score_head, qk_head = step + 2, step + LEAD, step + LEAD + 1, step + LEAD + 2, step + LEAD + 3
                 if step == x_step:
                     quantise_activations()
@@ -392,7 +396,7 @@ def tile_causalselfattention_pb_kernel(tc, x, Wv, vi, lamb, q_rot, k_rot, out):
                 if live(score_head):
                     scores(score_head, ((3,),))
                 if live(exp_head):
-                    exponentials(exp_head, (0, 1, 2, 3))
+                    exponentials(exp_head, (3, 1, 2, 0))
                 if live(step + 1):
                     scale_residual(step + 1)
                 v_grouped = mix_values(step) if live(step) else None
@@ -402,9 +406,30 @@ def tile_causalselfattention_pb_kernel(tc, x, Wv, vi, lamb, q_rot, k_rot, out):
                     quantise_values(step, v_grouped)
                 if live(score_head):
                     maxima(score_head, (0, 2, 1, 3))
-                if live(w_head) or live(e_head):
+                if w_head == last:
+                    quantise_weights_and_probabilities(w_head, HEADS, grouped)
+                    quantise_weights_and_probabilities(HEADS, e_head, grouped)
+                elif live(w_head) or live(e_head):
                     quantise_weights_and_probabilities(w_head, e_head, grouped)
                 if live(step + 1):
                     project_values(step + 1)
                 if live(step):
                     attend(step)
+                if w_head == last:
+                    project_values(last)
+
+            grouped = new_grouped()
+            e_banks = transpose_probabilities(last)
+            for pair in range(2):
+                copy_words(e_banks[pair], grouped[:, 1, :], pair)
+            scale_residual(last)
+            v_grouped = mix_values(last - 1)
+            normalise_and_store(last - 2)
+            quantise_values(last - 1, v_grouped)
+            attend(last - 1)
+            v_grouped = mix_values(last)
+            quantise_values(last, v_grouped)
+            normalise_and_store(last - 1)
+            quantise_weights_and_probabilities(HEADS, last, grouped)
+            attend(last)
+            normalise_and_store(last, parts=2)

from contextlib import ExitStack

import concourse.masks as masks
import concourse.mybir as mybir

F32 = mybir.dt.float32
BF16 = mybir.dt.bfloat16
U32 = mybir.dt.uint32
U8 = mybir.dt.uint8
FP8X4 = mybir.dt.float8_e4m3fn_x4
ALU = mybir.AluOpType
ACT = mybir.ActivationFunctionType
AXIS = mybir.AxisListType
ENGINE = mybir.EngineType

P = 128
PACK = 4
K_PASS = P * PACK
TOKENS = 512
DIM = 2048
HEADS = 16
HEAD_DIM = 128
TOKEN_TILES = TOKENS // P
K_PASSES = DIM // K_PASS
WORDS = K_PASS // 2
TURNING_BANKS = 7
MIX_BUFFERS = 5
BANK = 512
SCALE = HEAD_DIM ** -0.5
MASKED = -1.0e30

HEADS_PER_LOAD = 4
LOAD_COLS = HEADS_PER_LOAD * HEAD_DIM

LEAD = 1
E_TILES = 3

FLOPS = 2 * TOKENS * DIM * DIM + 2 * 2 * HEADS * TOKENS * TOKENS * HEAD_DIM


def tile_causalselfattention_pb_kernel(tc, x, Wv, vi, lamb, q_rot, k_rot, out):
    nc = tc.nc
    with ExitStack() as ctx:
        consts = ctx.enter_context(tc.tile_pool(name="consts", bufs=1))
        inputs = ctx.enter_context(tc.tile_pool(name="inputs", bufs=1))
        x_mx = ctx.enter_context(tc.tile_pool(name="x_mx", bufs=1))
        grouped_pool = ctx.enter_context(tc.tile_pool(name="grouped", bufs=3))
        pair_mx = ctx.enter_context(tc.tile_pool(name="pair_mx", bufs=LEAD + 3))
        v_mx = ctx.enter_context(tc.tile_pool(name="v_mx", bufs=3))
        qk_pool = ctx.enter_context(tc.tile_pool(name="qk", bufs=3))
        scaled_pool = ctx.enter_context(tc.tile_pool(name="scaled", bufs=2))
        rows = ctx.enter_context(tc.tile_pool(name="rows", bufs=LEAD + 5))
        y_pool = ctx.enter_context(tc.tile_pool(name="y", bufs=HEADS))
        w_pool = ctx.enter_context(tc.tile_pool(name="w_raw", bufs=HEADS // 2))
        mix_pool = ctx.enter_context(tc.tile_pool(name="mix", bufs=1))
        mix_taken = []

        def new_mix_buffer(dtype):
            turn = "mix%d" % (len(mix_taken) % MIX_BUFFERS)
            mix_taken.append(turn)
            return mix_pool.tile([P, HEAD_DIM, PACK], dtype, name=turn, tag=turn, align_bytes=64)

        banks = ctx.enter_context(tc.psum_pool(name="banks", bufs=1))
        kept_bank = banks.tile([P, 2, 2, P], F32, name="kept_bank", tag="kept_bank")
        banks_taken = []

        def new_bank(shape, dtype):
            turn = "bank%d" % (len(banks_taken) % TURNING_BANKS)
            banks_taken.append(turn)
            return banks.tile(shape, dtype, name=turn, tag=turn)

        q_view = q_rot.rearrange("(i p) h d -> p i (h d)", p=P)
        k_view = k_rot.rearrange("(i p) h d -> p i (h d)", p=P)
        x_view = x.rearrange("(half p odd) k -> p half (odd k)", half=2, odd=2)
        vi_view = vi.rearrange("(half p odd) h d -> p half odd (h d)", half=2, odd=2)
        out_view = out.rearrange("(i p) h d -> p i h d", p=P)

        lamb_bf16 = consts.tile([P, 1], BF16, name="lamb_bf16")
        nc.scalar.dma_start(out=lamb_bf16[:], in_=lamb.partition_broadcast(P))

        x_raw = inputs.tile([P, TOKEN_TILES * DIM], BF16, name="x_raw")
        q_raw, k_raw, vi_raw, w_raw = {}, {}, {}, {}

        def starts_a_load(head):
            return 0 <= head < HEADS and head % HEADS_PER_LOAD == 0

        first_step = -(LEAD + 3)
        last_step = HEADS + 1
        x_step = -2

        for step in range(first_step, last_step):
            head = step + LEAD + 3
            if starts_a_load(head):
                group = head // HEADS_PER_LOAD
                cols = slice(group * LOAD_COLS, (group + 1) * LOAD_COLS)
                q_raw[group] = inputs.tile([P, TOKEN_TILES, LOAD_COLS], BF16, name="q_raw%d" % group)
                k_raw[group] = inputs.tile([P, TOKEN_TILES, LOAD_COLS], BF16, name="k_raw%d" % group)
                nc.sync.dma_start(out=q_raw[group][:], in_=q_view[:, :, cols])
                nc.sync.dma_start(out=k_raw[group][:], in_=k_view[:, :, cols])
            if step == x_step:
                x_halves = x_raw[:].rearrange("p (half r) -> p half r", half=2)
                for half in range(2):
                    nc.sync.dma_start(out=x_halves[:, half, :], in_=x_view[:, half, :])
            head = step + 2
            if 0 <= head < HEADS:
                w_raw[head] = w_pool.tile([P, DIM], BF16, name="w_raw")
                nc.sync.dma_start(out=w_raw[head][:], in_=Wv[head * P : (head + 1) * P, :])
            head = step + 1
            if starts_a_load(head):
                group = head // HEADS_PER_LOAD
                cols = slice(group * LOAD_COLS, (group + 1) * LOAD_COLS)
                vi_raw[group] = inputs.tile([P, PACK, LOAD_COLS], BF16, name="vi_raw%d" % group)
                for half in range(2):
                    nc.sync.dma_start(
                        out=vi_raw[group][:, 2 * half : 2 * half + 2, :],
                        in_=vi_view[:, half, :, cols],
                    )

        ident_f32 = consts.tile([P, P], F32, name="ident_f32")
        masks.make_identity(nc, ident_f32[:])
        ident_bf16 = consts.tile([P, P], BF16, name="ident_bf16")
        masks.make_identity(nc, ident_bf16[:])
        mask_f32 = consts.tile([P, P], F32, name="mask_f32")
        nc.gpsimd.memset(mask_f32[:], 0.0)
        nc.gpsimd.affine_select(
            out=mask_f32[:],
            in_=mask_f32[:],
            compare_op=ALU.is_ge,
            fill=MASKED,
            base=0,
            pattern=[[-1, P]],
            channel_multiplier=1,
        )
        e_tiles = []
        for n in range(E_TILES):
            e_tile = consts.tile([P, TOKEN_TILES * TOKENS], BF16, name="e_tile%d" % n)
            nc.vector.memset(e_tile[:], 0.0)
            e_tiles.append(e_tile)
        future_mask = consts.tile([P, P], BF16, name="future_mask")
        nc.vector.tensor_copy(out=future_mask[:], in_=mask_f32[:])
        lam = consts.tile([P, 1], F32, name="lam")
        nc.vector.tensor_copy(out=lam[:], in_=lamb_bf16[:])
        one_minus_lam = consts.tile([P, 1], F32, name="one_minus_lam")
        nc.vector.tensor_scalar(
            out=one_minus_lam[:], in0=lam[:], scalar1=-1.0, scalar2=1.0, op0=ALU.mult, op1=ALU.add
        )

        def new_grouped():
            return grouped_pool.tile([P, 2, PACK * BANK], BF16, name="grouped", align_bytes=64)

        def transpose_words(source_words, pair, bank, halves=(0, 1)):
            for run in range(2):
                for half in halves:
                    nc.tensor.transpose(
                        bank[:, run, half, :],
                        source_words[:, 2 * pair + run, half * P : (half + 1) * P],
                        ident_f32[:],
                    )
            return bank

        def copy_words(bank, grouped, pair, copy=nc.scalar.copy):
            grouped_words = grouped.bitcast(F32).rearrange(
                "p (run row half) -> p run row half", run=4, half=2
            )
            copy(
                out=grouped_words[:, 2 * pair : 2 * pair + 2],
                in_=bank[:].rearrange("p run half row -> p run row half"),
            )

        def quantise(grouped, codes, scales):
            nc.vector.quantize_mx(out=codes.bitcast(FP8X4), scales=scales, in_=grouped)

        x_codes = x_mx.tile([P, K_PASSES, TOKENS], U32, name="x_codes", align_bytes=64)
        x_scales = x_mx.tile([P, K_PASSES, TOKENS], U8, name="x_scales", align_bytes=64)

        def quantise_activations():
            x_words = x_raw[:].bitcast(F32).rearrange("p (j w) -> p j w", j=TOKEN_TILES)
            grouped = [new_grouped() for first in range(0, K_PASSES, 2)]
            for half in range(2):
                for c in range(K_PASSES):
                    bank = new_bank([P, 2, 2, P], F32)
                    transpose_words(x_words[:, :, c * WORDS : (c + 1) * WORDS], half, bank)
                    copy = (nc.scalar.copy, nc.vector.tensor_copy)[c % 2]
                    copy_words(bank, grouped[c // 2][:, c % 2, :], half, copy)
            for n, first in enumerate(range(0, K_PASSES, 2)):
                quantise(
                    grouped[n][:].rearrange("p n w -> p (n w)"),
                    x_codes[:, first : first + 2, :].rearrange("p c t -> p (c t)"),
                    x_scales[:, first : first + 2, :].rearrange("p c t -> p (c t)"),
                )

        zero_words = e_tiles[0][:].bitcast(F32).rearrange("p (i w) -> p i w", i=TOKEN_TILES)
        transpose_words(zero_words, 0, kept_bank, halves=(1,))

        w_codes, w_scales = {}, {}
        qk_t = {}
        e_codes, e_scales = {}, {}
        scaled, shift, row_sum, row_scale = {}, {}, {}, {}
        residual, v_sum, v_codes, v_scales = {}, {}, {}, {}
        y_sum = {}

        def transpose_weights(head):
            w_words = w_raw[head][:].bitcast(F32).rearrange("p (c w) -> p c w", c=K_PASSES)
            return [transpose_words(w_words, pair, new_bank([P, 2, 2, P], F32)) for pair in range(2)]

        def quantise_weights_and_probabilities(w_head, e_head, grouped):
            codes = pair_mx.tile([P, 2, BANK], U32, name="pair_codes", align_bytes=64)
            scales = pair_mx.tile([P, 2, BANK], U8, name="pair_scales", align_bytes=64)
            first = 0 if live(w_head) else 1
            last = 2 if live(e_head) else 1
            quantise(
                grouped[:, first:last, :].rearrange("p n w -> p (n w)"),
                codes[:, first:last, :].rearrange("p n w -> p (n w)"),
                scales[:, first:last, :].rearrange("p n w -> p (n w)"),
            )
            w_codes[w_head], w_scales[w_head] = codes[:, 0, :], scales[:, 0, :]
            e_codes[e_head], e_scales[e_head] = codes[:, 1, :], scales[:, 1, :]
            if live(e_head):
                row_scale[e_head] = rows.tile([P, TOKEN_TILES], F32, name="row_scale")
                nc.vector.reciprocal(out=row_scale[e_head][:], in_=row_sum[e_head][:])

        def project_values(head):
            v_sum[head] = new_bank([P, PACK, HEAD_DIM], F32)
            for j in range(TOKEN_TILES):
                for c in range(K_PASSES):
                    tokens = slice(j * P, (j + 1) * P)
                    features = slice(c * HEAD_DIM, (c + 1) * HEAD_DIM)
                    nc.tensor.matmul_mx(
                        out=v_sum[head][:, j, :],
                        lhsT=x_codes[:, c, tokens].bitcast(FP8X4),
                        lhsT_scale=x_scales[:, c, tokens],
                        rhs=w_codes[head][:, features].bitcast(FP8X4),
                        rhs_scale=w_scales[head][:, features],
                        start=(c == 0),
                        stop=(c == K_PASSES - 1),
                    )

        def scale_residual(head):
            group = head // HEADS_PER_LOAD
            cols = slice((head % HEADS_PER_LOAD) * HEAD_DIM, (head % HEADS_PER_LOAD + 1) * HEAD_DIM)
            residual[head] = new_mix_buffer(F32)
            nc.gpsimd.tensor_scalar(
                out=residual[head][:],
                in0=vi_raw[group][:, :, cols].rearrange("p j d -> p d j"),
                scalar1=lam[:, 0:1],
                scalar2=0.0,
                op0=ALU.mult,
                op1=ALU.add,
            )

        def mix_values(head):
            v_grouped = new_mix_buffer(BF16)
            nc.vector.scalar_tensor_tensor(
                out=v_grouped[:],
                in0=v_sum[head][:].rearrange("p j d -> p d j"),
                scalar=one_minus_lam[:, 0:1],
                in1=residual[head][:],
                op0=ALU.mult,
                op1=ALU.add,
            )
            return v_grouped

        def quantise_values(head, v_grouped):
            v_codes[head] = v_mx.tile([P, HEAD_DIM], U32, name="v_codes", align_bytes=64)
            v_scales[head] = v_mx.tile([P, HEAD_DIM], U8, name="v_scales", align_bytes=64)
            nc.vector.quantize_mx(
                out=v_codes[head][:].bitcast(FP8X4),
                scales=v_scales[head][:],
                in_=v_grouped[:].rearrange("p d j -> p (d j)"),
            )

        def transpose_queries_keys(head):
            group = head // HEADS_PER_LOAD
            cols = slice((head % HEADS_PER_LOAD) * HEAD_DIM, (head % HEADS_PER_LOAD + 1) * HEAD_DIM)
            bank = new_bank([P, 2, TOKENS], BF16)
            for which, raw in enumerate((q_raw[group], k_raw[group])):
                for i in range(TOKEN_TILES):
                    nc.tensor.transpose(bank[:, which, i * P : (i + 1) * P], raw[:, i, cols], ident_bf16[:])
            return bank

        def copy_queries_keys(head, bank):
            qk_t[head] = qk_pool.tile([P, 2, TOKENS], BF16, name="qk_t")
            nc.scalar.copy(out=qk_t[head][:], in_=bank[:])

        score = {}

        def scores(head, tile_groups):
            for tiles in tile_groups:
                bank = new_bank([P, BANK], F32)
                first_col = 0
                for i in tiles:
                    keys = (i + 1) * P
                    score[head, i] = bank[:, first_col : first_col + keys]
                    first_col += keys
                    nc.tensor.matmul(
                        out=score[head, i],
                        lhsT=qk_t[head][:, 0, i * P : (i + 1) * P],
                        rhs=qk_t[head][:, 1, 0:keys],
                        start=True,
                        stop=False,
                    )
                    nc.tensor.matmul(
                        out=score[head, i][:, keys - P : keys],
                        lhsT=ident_bf16[:],
                        rhs=future_mask[:],
                        start=False,
                        stop=True,
                    )

        def maxima(head, tiles):
            if head not in shift:
                shift[head] = rows.tile([P, TOKEN_TILES], F32, name="shift")
                scaled[head] = {}
            for i in tiles:
                scaled[head][i] = scaled_pool.tile([P, (i + 1) * P], F32, name="scaled%d" % i)
                nc.vector.tensor_scalar(
                    out=scaled[head][i][:],
                    in0=score[head, i],
                    scalar1=-SCALE,
                    scalar2=None,
                    op0=ALU.mult,
                    op1=ALU.min,
                    accum_out=shift[head][:, i : i + 1],
                )

        def exponentials(head, tiles):
            if head not in row_sum:
                row_sum[head] = rows.tile([P, TOKEN_TILES], F32, name="row_sum")
            e_rows = e_tiles[head % E_TILES][:].rearrange("p (i u) -> p i u", i=TOKEN_TILES)
            for i in tiles:
                nc.scalar.activation(
                    out=e_rows[:, i, 0 : (i + 1) * P],
                    in_=scaled[head][i][:],
                    func=ACT.Exp,
                    bias=shift[head][:, i : i + 1],
                    scale=-1.0,
                    accum_out=row_sum[head][:, i : i + 1],
                )

        def transpose_probabilities(head):
            e_words = e_tiles[head % E_TILES][:].bitcast(F32).rearrange("p (i w) -> p i w", i=TOKEN_TILES)
            return [
                transpose_words(e_words, 0, kept_bank, halves=(0,)),
                transpose_words(e_words, 1, new_bank([P, 2, 2, P], F32)),
            ]

        def attend(head):
            y_sum[head] = new_bank([P, TOKEN_TILES, HEAD_DIM], F32)
            for i in range(TOKEN_TILES):
                queries = slice(i * P, (i + 1) * P)
                nc.tensor.matmul_mx(
                    out=y_sum[head][:, i, :],
                    lhsT=e_codes[head][:, queries].bitcast(FP8X4),
                    lhsT_scale=e_scales[head][:, queries],
                    rhs=v_codes[head][:].bitcast(FP8X4),
                    rhs_scale=v_scales[head][:],
                    start=True,
                    stop=True,
                )

        def normalise_and_store(head, parts=1):
            y = y_pool.tile([P, TOKEN_TILES, HEAD_DIM], F32, name="y")
            count = TOKEN_TILES // parts
            for first in range(0, TOKEN_TILES, count):
                tiles = slice(first, first + count)
                nc.vector.tensor_tensor(
                    out=y[:, tiles, :],
                    in0=y_sum[head][:, tiles, :],
                    in1=row_scale[head][:, tiles].unsqueeze(2).to_broadcast([P, count, HEAD_DIM]),
                    op=ALU.mult,
                )
                nc.sync.dma_start(out=out_view[:, tiles, head, :], in_=y[:, tiles, :])

        def live(head):
            return 0 <= head < HEADS

        with tc.manual_schedule(engines={ENGINE.PE, ENGINE.Activation, ENGINE.DVE}):
            last = HEADS - 1
            for step in range(first_step, last - 1):
                w_head, e_head, exp_head, score_head, qk_head = step + 2, step + LEAD, step + LEAD + 1, step + LEAD + 2, step + LEAD + 3
                if step == x_step:
                    quantise_activations()
                grouped = new_grouped() if live(w_head) or live(e_head) else None
                if live(w_head):
                    w_banks = transpose_weights(w_head)
                    for pair in range(2):
                        copy_words(w_banks[pair], grouped[:, 0, :], pair)
                if live(qk_head):
                    copy_queries_keys(qk_head, transpose_queries_keys(qk_head))
                if live(score_head):
                    scores(score_head, ((0, 2), (1,)))
                if live(e_head):
                    e_banks = transpose_probabilities(e_head)
                    for pair in range(2):
                        copy_words(e_banks[pair], grouped[:, 1, :], pair)
                if live(score_head):
                    scores(score_head, ((3,),))
                if live(exp_head):
                    exponentials(exp_head, (3, 1, 2, 0))
                if live(step + 1):
                    scale_residual(step + 1)
                v_grouped = mix_values(step) if live(step) else None
                if live(step - 1):
                    normalise_and_store(step - 1)
                if live(step):
                    quantise_values(step, v_grouped)
                if live(score_head):
                    maxima(score_head, (0, 2, 1, 3))
                if w_head == last:
                    quantise_weights_and_probabilities(w_head, HEADS, grouped)
                    quantise_weights_and_probabilities(HEADS, e_head, grouped)
                elif live(w_head) or live(e_head):
                    quantise_weights_and_probabilities(w_head, e_head, grouped)
                if live(step + 1):
                    project_values(step + 1)
                if live(step):
                    attend(step)
                if w_head == last:
                    project_values(last)

            grouped = new_grouped()
            e_banks = transpose_probabilities(last)
            for pair in range(2):
                copy_words(e_banks[pair], grouped[:, 1, :], pair)
            scale_residual(last)
            v_grouped = mix_values(last - 1)
            normalise_and_store(last - 2)
            quantise_values(last - 1, v_grouped)
            attend(last - 1)
            v_grouped = mix_values(last)
            quantise_values(last, v_grouped)
            normalise_and_store(last - 1)
            quantise_weights_and_probabilities(HEADS, last, grouped)
            attend(last)
            normalise_and_store(last, parts=2)
